import numpy as np
import ml_dtypes


def mxq(x, axis, fmt="e4m3"):
    dtype, down = {"e4m3": (ml_dtypes.float8_e4m3fn, 7), "e5m2": (ml_dtypes.float8_e5m2, 14)}[fmt]
    v = np.moveaxis(np.asarray(x, np.float32).astype(ml_dtypes.bfloat16).astype(np.float64), axis, -1)
    blocks = v.reshape(v.shape[:-1] + (-1, 32))
    amax = np.abs(blocks).max(-1, keepdims=True)
    byte = np.maximum(np.where(amax > 0, np.frexp(amax)[1] - 1 + 127, 0) - down, 1)
    scale = np.exp2(byte - 127.0)
    codes = (blocks / scale).astype(np.float32).astype(dtype).astype(np.float64)
    return np.moveaxis((codes * scale).reshape(v.shape), -1, axis)


WIDE = False


def mx_kscale(k):
    if not WIDE:
        return np.ones(k)
    levels = np.array([20, -20, 10, -10, 0])
    a = np.random.permutation(np.resize(levels, k // 512 * 4)).reshape(k // 512, 4)
    idx = np.arange(k)
    return np.exp2(a[idx // 512, idx % 128 // 32])


BF16 = ml_dtypes.bfloat16


def bf(x):
    return np.asarray(x, np.float32).astype(BF16)


def f64(x):
    return np.asarray(x).astype(np.float64)


B, I, H = 4096, 512, 128
EPS = 1e-5


def sigmoid(v):
    return 1.0 / (1.0 + np.exp(-v))


def setup_inputs():
    rn = np.random.standard_normal
    u = mx_kscale(4 * H)
    x = bf(rn((B, I)))
    c = bf(rn((B, H)))
    h = bf(rn((B, H)))
    w_ih0 = bf(rn((4 * H, I)) / np.sqrt(I))
    w_hh = bf(rn((4 * H, H)) / np.sqrt(H))
    b = bf(0.3 * rn(4 * H))
    g_ih0 = bf(1.0 + 0.1 * rn(4 * H))
    b_ih = bf(0.3 * rn(4 * H))
    g_hh = bf(1.0 + 0.1 * rn(4 * H))
    b_hh = bf(0.3 * rn(4 * H))
    g_c = bf(1.0 + 0.1 * rn(H))
    b_c = bf(0.3 * rn(H))
    grad_out = bf(rn((2, B, H)) * np.exp2(np.random.randint(-12, 1, (1, B, 1))) * 16.0)
    a = f64(x) @ f64(w_ih0).T
    ih_rstd = 1.0 / np.sqrt(np.var(a, axis=0) + EPS)
    ih_hat = (a - np.mean(a, axis=0)) * ih_rstd
    a2 = f64(h) @ f64(w_hh).T
    hh_hat = (a2 - np.mean(a2, axis=0)) / np.sqrt(np.var(a2, axis=0) + EPS)
    gates = ih_hat * f64(g_ih0) + f64(b_ih) + hh_hat * f64(g_hh) + f64(b_hh) + f64(b)
    return {"x": x, "c": c, "h": h,
            "w_ih": bf(f64(w_ih0) / u[:, None]),
            "w_hh": w_hh, "b": b,
            "g_ih": bf(f64(g_ih0) * u),
            "b_ih": b_ih, "g_hh": g_hh, "b_hh": b_hh, "g_c": g_c, "b_c": b_c,
            "gates": np.asarray(gates, np.float32),
            "ih_hat": np.asarray(ih_hat, np.float32),
            "ih_rstd": np.asarray(ih_rstd, np.float32),
            "grad_out": grad_out}


def reference(x, c, h, w_ih, w_hh, b, g_ih, b_ih, g_hh, b_hh, g_c, b_c, gates, ih_hat, ih_rstd, grad_out):
    zf, zi, zo, zg = np.split(f64(gates), 4, axis=1)
    f = sigmoid(zf)
    i = sigmoid(zi)
    o = sigmoid(zo)
    g = np.tanh(zg)
    cf = f64(c)
    v = f * cf + i * g
    r = 1.0 / np.sqrt(np.var(v, axis=0) + EPS)
    c_hat = (v - np.mean(v, axis=0)) * r
    tc = np.tanh(c_hat * f64(g_c) + f64(b_c))
    go = f64(grad_out)
    g0 = go[0]
    g1 = go[1]
    dcn = g0 + g1 * o * (1.0 - tc * tc)
    dv = (f64(g_c) * r) * (dcn - np.mean(dcn, axis=0) - c_hat * np.mean(dcn * c_hat, axis=0))
    dgates = np.concatenate([dv * cf * f * (1.0 - f),
                             dv * g * i * (1.0 - i),
                             g1 * tc * o * (1.0 - o),
                             dv * i * (1.0 - g * g)], axis=1)
    xh = f64(ih_hat)
    da = (f64(g_ih) * f64(ih_rstd)) * (dgates - np.mean(dgates, axis=0) - xh * np.mean(dgates * xh, axis=0))
    return mxq(da, 1, "e5m2") @ mxq(f64(w_ih), 0, "e4m3")

@@ -1,0 +1,328 @@
+from contextlib import ExitStack
+
+import concourse.mybir as mybir
+from concourse.masks import make_identity
+
+F32 = mybir.dt.float32
+BF16 = mybir.dt.bfloat16
+U32 = mybir.dt.uint32
+U8 = mybir.dt.uint8
+E4M3X4 = mybir.dt.float8_e4m3fn_x4
+E5M2X4 = mybir.dt.float8_e5m2_x4
+ACT = mybir.ActivationFunctionType
+ALU = mybir.AluOpType
+AX = mybir.AxisListType
+
+P = 128
+BATCH = 4096
+HID = 128
+KINDS = 4
+GATES = KINDS * HID
+WIDTH = 512
+ROWS = BATCH // P
+SL = 4
+CH = SL * P
+NCH = ROWS // SL
+EPS = 1e-5
+F_, I_, O_, G_ = 0, 1, 2, 3
+
+FLOPS = 2 * BATCH * GATES * WIDTH
+BYTES = 4 * 3 * BATCH * GATES + 2 * 3 * BATCH * HID + 2 * GATES * WIDTH + 6 * GATES + 4 * HID
+
+
+def tile_lstmcell_t_v_kernel(
+    tc, x, c, h, w_ih, w_hh, b, g_ih, b_ih, g_hh, b_hh, g_c, b_c, gates, ih_hat, ih_rstd, grad_out, out
+):
+    nc = tc.nc
+    gates_v = gates.rearrange("(p t) k -> p t k", t=ROWS)
+    xhat_v = ih_hat.rearrange("(p t) k -> p t k", t=ROWS)
+    c_v = c.rearrange("(p t) k -> p t k", t=ROWS)
+    grad_v = grad_out.rearrange("s (p t) k -> p s t k", t=ROWS)
+    out_v = out.rearrange("(p t) k -> p t k", t=ROWS)
+
+    def stt(out_ap, in0, scalar, op0, in1, op1, accum=None):
+        nc.vector.scalar_tensor_tensor(
+            out=out_ap, in0=in0, scalar=scalar, in1=in1, op0=op0, op1=op1, accum_out=accum
+        )
+
+    def transpose_slices(dst, src_of_slice, ident):
+        for s in range(SL):
+            nc.tensor.transpose(dst[:, s * P : (s + 1) * P], src_of_slice(s), ident[:])
+
+    with ExitStack() as stack:
+        stack.enter_context(tc.manual_schedule())
+        keep = stack.enter_context(tc.tile_pool(name="keep", bufs=1))
+        psum = stack.enter_context(tc.psum_pool(name="psum", bufs=4))
+
+        ident_f = keep.tile([P, P], F32)
+        make_identity(nc, ident_f[:])
+        ident_b = keep.tile([P, P], BF16)
+        make_identity(nc, ident_b[:])
+        rows_b = keep.tile([P, P], BF16)
+        nc.vector.memset(rows_b[:], 0.0)
+        rows_f = keep.tile([P, P], F32)
+        nc.vector.memset(rows_f[:], 0.0)
+        neg_half = keep.tile([P, 1], F32)
+        nc.vector.memset(neg_half[:], -0.5)
+        warm = keep.tile([P, 1], F32)
+        nc.scalar.dma_start(out=rows_b[0:KINDS, :], in_=g_ih.rearrange("(t p) -> t p", p=P))
+        nc.scalar.dma_start(out=rows_b[4:5, :], in_=g_c.rearrange("(o p) -> o p", o=1))
+        nc.scalar.dma_start(out=rows_b[5:6, :], in_=b_c.rearrange("(o p) -> o p", o=1))
+        nc.scalar.dma_start(out=rows_f[0:KINDS, :], in_=ih_rstd.rearrange("(t p) -> t p", p=P))
+        nc.scalar.activation(out=warm[:], in_=neg_half[:], func=ACT.Sigmoid)
+
+        cols_b = psum.tile([P, P], BF16, tag="rest")
+        nc.tensor.transpose(cols_b[:], rows_b[:], ident_b[:])
+        cols_f = psum.tile([P, P], F32, tag="wide")
+        nc.tensor.transpose(cols_f[:], rows_f[:], ident_f[:])
+        vecs = keep.tile([P, 6], F32)
+        nc.vector.tensor_copy(out=vecs[:], in_=cols_b[:, 0:6])
+        gamma_c = vecs[:, 4:5]
+        beta_c = vecs[:, 5:6]
+        gain_neg = keep.tile([P, KINDS], F32)
+        stt(gain_neg[:], vecs[:, 0:KINDS], -1.0, ALU.mult, cols_f[:, 0:KINDS], ALU.mult)
+
+        fac = keep.tile([P, KINDS, BATCH], F32)
+        xhat = keep.tile([P, ROWS, GATES], F32)
+        w_nat = keep.tile([P, KINDS, WIDTH], BF16)
+        w_codes = keep.tile([P, WIDTH], U32, align_bytes=64)
+        w_scales = keep.tile([P, WIDTH], U8, align_bytes=64)
+        sum_v = keep.tile([P, NCH], F32)
+        chunk_mean_neg = keep.tile([P, NCH], F32)
+        sq_parts = keep.tile([P, NCH], F32)
+        parts2 = keep.tile([P, 2, NCH], F32)
+        parts3 = keep.tile([P, 2 * KINDS, NCH], F32)
+        mean_neg = keep.tile([P, 1], F32)
+        a_tc = keep.tile([P, 1], F32)
+        b_tc = keep.tile([P, 1], F32)
+        coef2 = keep.tile([P, 2], F32)
+        lin2 = keep.tile([P, 2], F32)
+        c_lin = keep.tile([P, 1], F32)
+        neg3 = keep.tile([P, 2 * KINDS], F32)
+
+
+        with tc.tile_pool(name="mid", bufs=1) as mid:
+            cell = mid.tile([P, BATCH], F32)
+            dcn = mid.tile([P, BATCH], F32)
+            g0_nat = mid.tile([P, ROWS, HID], BF16)
+
+            with tc.tile_pool(name="p1", bufs=2) as p1:
+                acts = {}
+
+                def cell_value(j):
+                    sl = slice(j * SL, (j + 1) * SL)
+                    cols = slice(j * CH, (j + 1) * CH)
+                    z_nat = p1.tile([P, SL, GATES], F32, bufs=3)
+                    nc.sync.dma_start(out=z_nat[:], in_=gates_v[:, sl, :])
+                    c_nat = p1.tile([P, SL, HID], BF16, bufs=3)
+                    nc.sync.dma_start(out=c_nat[:], in_=c_v[:, sl, :])
+                    g1_nat = p1.tile([P, SL, HID], BF16, bufs=3)
+                    nc.sync.dma_start(out=g1_nat[:], in_=grad_v[:, 1, sl, :])
+
+                    cg = psum.tile([P, 2, CH], BF16, tag="rest")
+                    transpose_slices(cg[:, 0, :], lambda s: c_nat[:, s, :], ident_b)
+                    transpose_slices(cg[:, 1, :], lambda s: g1_nat[:, s, :], ident_b)
+                    gate = {}
+                    for kind in (F_, I_, G_, O_):
+                        z = psum.tile([P, CH], F32, tag="wide")
+                        transpose_slices(z, lambda s: z_nat[:, s, kind * HID : (kind + 1) * HID], ident_f)
+                        gate[kind] = p1.tile([P, CH], F32, name="gate%d" % kind)
+                        func = ACT.Tanh if kind == G_ else ACT.Sigmoid
+                        nc.scalar.activation(out=gate[kind][:], in_=z[:], func=func)
+                    g_sq = p1.tile([P, CH], F32)
+                    nc.scalar.activation(out=g_sq[:], in_=gate[G_][:], func=ACT.Square)
+
+                    nc.vector.tensor_tensor(out=fac[:, F_, cols], in0=gate[F_][:], in1=cg[:, 0, :], op=ALU.mult)
+                    nc.vector.tensor_tensor(out=fac[:, I_, cols], in0=gate[I_][:], in1=gate[G_][:], op=ALU.mult)
+                    stt(cell[:, cols], fac[:, F_, cols], 1.0, ALU.mult, fac[:, I_, cols], ALU.add, sum_v[:, j : j + 1])
+                    nc.vector.tensor_scalar_mul(
+                        out=chunk_mean_neg[:, j : j + 1], in0=sum_v[:, j : j + 1], scalar1=-1.0 / CH
+                    )
+                    sq_junk = p1.tile([P, CH], BF16)
+                    nc.scalar.activation(
+                        out=sq_junk[:], in_=cell[:, cols], func=ACT.Square,
+                        bias=chunk_mean_neg[:, j : j + 1], scale=1.0, accum_out=sq_parts[:, j : j + 1],
+                    )
+                    acts[j] = (gate, g_sq, cg)
+
+                def gate_factors(j):
+                    cols = slice(j * CH, (j + 1) * CH)
+                    gate, g_sq, cg = acts[j]
+                    nc.vector.tensor_tensor(out=dcn[:, cols], in0=gate[O_][:], in1=cg[:, 1, :], op=ALU.mult)
+                    stt(fac[:, F_, cols], gate[F_][:], 1.0, ALU.subtract, fac[:, F_, cols], ALU.mult)
+                    stt(fac[:, I_, cols], gate[I_][:], 1.0, ALU.subtract, fac[:, I_, cols], ALU.mult)
+                    stt(fac[:, G_, cols], g_sq[:], 1.0, ALU.subtract, gate[I_][:], ALU.mult)
+                    stt(fac[:, O_, cols], gate[O_][:], 1.0, ALU.subtract, dcn[:, cols], ALU.mult)
+
+                for j in range(NCH):
+                    cell_value(j)
+                    if j < NCH - 1:
+                        gate_factors(j)
+
+                nc.sync.dma_start(out=g0_nat[:], in_=grad_v[:, 0, :, :])
+                nc.sync.dma_start(out=w_nat[:], in_=w_ih.rearrange("(t p) i -> p t i", p=P))
+                for j in range(NCH):
+                    sl = slice(j * SL, (j + 1) * SL)
+                    nc.sync.dma_start(out=xhat[:, sl, :], in_=xhat_v[:, sl, :])
+
+                tot_v = p1.tile([P, 1], F32)
+                nc.vector.reduce_sum(out=tot_v[:], in_=sum_v[:], axis=AX.X)
+                nc.vector.tensor_scalar_mul(out=mean_neg[:], in0=tot_v[:], scalar1=-1.0 / BATCH)
+                dev = p1.tile([P, NCH], F32)
+                nc.vector.tensor_scalar_sub(out=dev[:], in0=chunk_mean_neg[:], scalar1=mean_neg[:, 0:1])
+                dev_sq = p1.tile([P, NCH], F32)
+                between = p1.tile([P, 1], F32)
+                stt(dev_sq[:], dev[:], float(CH), ALU.mult, dev[:], ALU.mult, between[:])
+                within = p1.tile([P, 1], F32)
+                nc.vector.reduce_sum(out=within[:], in_=sq_parts[:], axis=AX.X)
+                spread = p1.tile([P, 1], F32)
+                nc.vector.tensor_tensor(out=spread[:], in0=between[:], in1=within[:], op=ALU.add)
+                var_eps = p1.tile([P, 1], F32)
+                nc.vector.tensor_scalar(
+                    out=var_eps[:], in0=spread[:], scalar1=1.0 / BATCH, scalar2=EPS, op0=ALU.mult, op1=ALU.add
+                )
+                rstd = p1.tile([P, 1], F32)
+                nc.gpsimd.tensor_tensor(out=rstd[:], in0=var_eps[:], in1=neg_half[:], op=ALU.pow)
+                nc.vector.tensor_tensor(out=a_tc[:], in0=rstd[:], in1=gamma_c, op=ALU.mult)
+                stt(b_tc[:], mean_neg[:], a_tc[:, 0:1], ALU.mult, beta_c, ALU.add)
+
+                gate_factors(NCH - 1)
+
+                rstd_sq = p1.tile([P, 1], F32)
+                nc.vector.tensor_tensor(out=rstd_sq[:], in0=rstd[:], in1=rstd[:], op=ALU.mult)
+                nc.vector.tensor_scalar_mul(out=coef2[:, 0:1], in0=a_tc[:], scalar1=-1.0 / BATCH)
+                nc.vector.tensor_tensor(out=coef2[:, 1:2], in0=coef2[:, 0:1], in1=rstd_sq[:], op=ALU.mult)
+
+            with tc.tile_pool(name="p23", bufs=2, reuse_waits="tile") as p23:
+                for j in range(NCH):
+                    cols = slice(j * CH, (j + 1) * CH)
+                    g0 = psum.tile([P, CH], BF16, tag="rest")
+                    transpose_slices(g0, lambda s: g0_nat[:, j * SL + s, :], ident_b)
+                    tanh_c = p23.tile([P, CH], F32)
+                    nc.scalar.activation(
+                        out=tanh_c[:], in_=cell[:, cols], func=ACT.Tanh, bias=b_tc[:, 0:1], scale=a_tc[:, 0:1]
+                    )
+                    through = p23.tile([P, CH], F32)
+                    nc.scalar.activation(out=through[:], in_=tanh_c[:], func=ACT.Square)
+                    stt(through[:], through[:], 1.0, ALU.subtract, dcn[:, cols], ALU.mult)
+                    stt(
+                        fac[:, O_, cols], tanh_c[:], gain_neg[:, O_ : O_ + 1], ALU.mult, fac[:, O_, cols], ALU.mult,
+                        parts3[:, O_, j : j + 1],
+                    )
+                    stt(dcn[:, cols], through[:], -1.0, ALU.mult, g0[:], ALU.add, parts2[:, 0, j : j + 1])
+                    junk = p23.tile([P, CH], F32)
+                    stt(junk[:], cell[:, cols], mean_neg[:, 0:1], ALU.add, dcn[:, cols], ALU.mult, parts2[:, 1, j : j + 1])
+
+                tot2 = p23.tile([P, 2], F32)
+                nc.vector.reduce_sum(out=tot2[:], in_=parts2[:], axis=AX.X)
+                nc.vector.tensor_tensor(out=lin2[:], in0=tot2[:], in1=coef2[:], op=ALU.mult)
+                stt(c_lin[:], lin2[:, 1:2], mean_neg[:, 0:1], ALU.mult, lin2[:, 0:1], ALU.add)
+
+                for j in range(NCH):
+                    cols = slice(j * CH, (j + 1) * CH)
+                    xt = {}
+                    for kind in (O_, F_, I_, G_):
+                        xt[kind] = psum.tile([P, CH], F32, tag="wide", name="xt%d" % kind)
+                        transpose_slices(
+                            xt[kind], lambda s: xhat[:, j * SL + s, kind * HID : (kind + 1) * HID], ident_f
+                        )
+                    dv = p23.tile([P, CH], F32)
+                    nc.scalar.activation(
+                        out=dv[:], in_=cell[:, cols], func=ACT.Identity, bias=c_lin[:, 0:1], scale=lin2[:, 1:2]
+                    )
+
+                    def times_xhat(kind):
+                        junk = p23.tile([P, CH], F32)
+                        stt(
+                            junk[:], fac[:, kind, cols], 1.0, ALU.mult, xt[kind][:], ALU.mult,
+                            parts3[:, KINDS + kind, j : j + 1],
+                        )
+
+                    times_xhat(O_)
+                    stt(dv[:], dcn[:, cols], a_tc[:, 0:1], ALU.mult, dv[:], ALU.add)
+                    for kind in (F_, I_, G_):
+                        stt(
+                            fac[:, kind, cols], dv[:], gain_neg[:, kind : kind + 1], ALU.mult, fac[:, kind, cols],
+                            ALU.mult, parts3[:, kind, j : j + 1],
+                        )
+                    for kind in (F_, I_, G_):
+                        times_xhat(kind)
+
+                tot3 = p23.tile([P, 2 * KINDS], F32)
+                nc.vector.reduce_sum(out=tot3[:], in_=parts3[:], axis=AX.X)
+                nc.vector.tensor_scalar_mul(out=neg3[:], in0=tot3[:], scalar1=-1.0 / BATCH)
+
+        with tc.tile_pool(name="p4", bufs=2) as p4:
+            shifts = {}
+            sums = {}
+
+            def shift_terms(j):
+                shift = p4.tile([P, KINDS, CH], F32)
+                for kind in range(KINDS):
+                    xt = psum.tile([P, CH], F32, tag="wide")
+                    transpose_slices(xt, lambda s: xhat[:, j * SL + s, kind * HID : (kind + 1) * HID], ident_f)
+                    nc.scalar.activation(
+                        out=shift[:, kind, :], in_=xt[:], func=ACT.Identity,
+                        bias=neg3[:, kind : kind + 1], scale=neg3[:, KINDS + kind : KINDS + kind + 1],
+                    )
+                shifts[j] = shift
+
+            def add_and_round(j):
+                cols = slice(j * CH, (j + 1) * CH)
+                da = p4.tile([P, CH, KINDS], BF16, align_bytes=64)
+                nc.vector.tensor_tensor(
+                    out=da[:].rearrange("p (c i) t -> p c t i", i=4),
+                    in0=fac[:, :, cols].rearrange("p t (c i) -> p c t i", i=4),
+                    in1=shifts[j][:].rearrange("p t (c i) -> p c t i", i=4),
+                    op=ALU.add,
+                )
+                return da
+
+            def quantise_and_multiply(j, da):
+                codes = p4.tile([P, CH], U32, align_bytes=64)
+                scales = p4.tile([P, CH], U8, align_bytes=64)
+                nc.vector.quantize_mx(
+                    out=codes[:].bitcast(E5M2X4), scales=scales[:], in_=da[:].rearrange("p b t -> p (b t)")
+                )
+                sums[j] = []
+                for s in range(SL):
+                    rows = slice(s * P, (s + 1) * P)
+                    acc = psum.tile([P, WIDTH], F32, tag="rest")
+                    nc.tensor.matmul_mx(
+                        out=acc[:],
+                        lhsT=codes[:, rows].bitcast(E5M2X4),
+                        lhsT_scale=scales[:, rows],
+                        rhs=w_codes[:].bitcast(E4M3X4),
+                        rhs_scale=w_scales[:],
+                        start=True,
+                        stop=True,
+                    )
+                    sums[j].append(acc)
+
+            def store(j):
+                result = p4.tile([P, SL, WIDTH], F32, bufs=3)
+                for s in range(SL):
+                    if s % 2 == 0:
+                        nc.scalar.copy(out=result[:, s, :], in_=sums[j][s][:])
+                    else:
+                        nc.vector.tensor_copy(out=result[:, s, :], in_=sums[j][s][:])
+                nc.sync.dma_start(out=out_v[:, j * SL : (j + 1) * SL, :], in_=result[:])
+
+            shift_terms(0)
+            w_grouped = p4.tile([P, WIDTH, KINDS], BF16, align_bytes=64, bufs=1)
+            nc.vector.tensor_copy(
+                out=w_grouped[:].rearrange("p (c i) t -> p c t i", i=4),
+                in_=w_nat[:].rearrange("p t (c i) -> p c t i", i=4),
+            )
+            nc.vector.quantize_mx(
+                out=w_codes[:].bitcast(E4M3X4), scales=w_scales[:], in_=w_grouped[:].rearrange("p i t -> p (i t)")
+            )
+            for j in range(NCH + 1):
+                if j + 1 < NCH:
+                    shift_terms(j + 1)
+                if j < NCH:
+                    da = add_and_round(j)
+                if j > 0:
+                    store(j - 1)
+                if j < NCH:
+                    quantise_and_multiply(j, da)

@@ -50,7 +50,6 @@ def tile_lstmcell_t_v_kernel(
             nc.tensor.transpose(dst[:, s * P : (s + 1) * P], src_of_slice(s), ident[:])
 
     with ExitStack() as stack:
-        stack.enter_context(tc.manual_schedule())
         keep = stack.enter_context(tc.tile_pool(name="keep", bufs=1))
         psum = stack.enter_context(tc.psum_pool(name="psum", bufs=4))
 

@@ -90,7 +90,9 @@ def tile_lstmcell_t_v_kernel(
         chunk_mean_neg = keep.tile([P, NCH], F32)
         sq_parts = keep.tile([P, NCH], F32)
         parts2 = keep.tile([P, 2, NCH], F32)
-        parts3 = keep.tile([P, 2 * KINDS, NCH], F32)
+        mean_parts_v = keep.tile([P, 2, NCH], F32)
+        mean_parts_s = keep.tile([P, 2, NCH], F32)
+        corr_parts = keep.tile([P, KINDS, NCH], F32)
         mean_neg = keep.tile([P, 1], F32)
         a_tc = keep.tile([P, 1], F32)
         b_tc = keep.tile([P, 1], F32)
@@ -122,7 +124,7 @@ def tile_lstmcell_t_v_kernel(
                     transpose_slices(cg[:, 0, :], lambda s: c_nat[:, s, :], ident_b)
                     transpose_slices(cg[:, 1, :], lambda s: g1_nat[:, s, :], ident_b)
                     gate = {}
-                    for kind in (F_, I_, G_, O_):
+                    for kind in (F_, O_, I_, G_):
                         z = psum.tile([P, CH], F32, tag="wide")
                         transpose_slices(z, lambda s: z_nat[:, s, kind * HID : (kind + 1) * HID], ident_f)
                         gate[kind] = p1.tile([P, CH], F32, name="gate%d" % kind)
@@ -132,7 +134,8 @@ def tile_lstmcell_t_v_kernel(
                     nc.scalar.activation(out=g_sq[:], in_=gate[G_][:], func=ACT.Square)
 
                     nc.vector.tensor_tensor(out=fac[:, F_, cols], in0=gate[F_][:], in1=cg[:, 0, :], op=ALU.mult)
-                    nc.vector.tensor_tensor(out=fac[:, I_, cols], in0=gate[I_][:], in1=gate[G_][:], op=ALU.mult)
+                    nc.gpsimd.tensor_tensor(out=fac[:, I_, cols], in0=gate[I_][:], in1=gate[G_][:], op=ALU.mult)
+                    nc.vector.tensor_tensor(out=dcn[:, cols], in0=gate[O_][:], in1=cg[:, 1, :], op=ALU.mult)
                     stt(cell[:, cols], fac[:, F_, cols], 1.0, ALU.mult, fac[:, I_, cols], ALU.add, sum_v[:, j : j + 1])
                     nc.vector.tensor_scalar_mul(
                         out=chunk_mean_neg[:, j : j + 1], in0=sum_v[:, j : j + 1], scalar1=-1.0 / CH
@@ -142,12 +145,11 @@ def tile_lstmcell_t_v_kernel(
                         out=sq_junk[:], in_=cell[:, cols], func=ACT.Square,
                         bias=chunk_mean_neg[:, j : j + 1], scale=1.0, accum_out=sq_parts[:, j : j + 1],
                     )
-                    acts[j] = (gate, g_sq, cg)
+                    acts[j] = (gate, g_sq)
 
                 def gate_factors(j):
                     cols = slice(j * CH, (j + 1) * CH)
-                    gate, g_sq, cg = acts[j]
-                    nc.vector.tensor_tensor(out=dcn[:, cols], in0=gate[O_][:], in1=cg[:, 1, :], op=ALU.mult)
+                    gate, g_sq = acts[j]
                     stt(fac[:, F_, cols], gate[F_][:], 1.0, ALU.subtract, fac[:, F_, cols], ALU.mult)
                     stt(fac[:, I_, cols], gate[I_][:], 1.0, ALU.subtract, fac[:, I_, cols], ALU.mult)
                     stt(fac[:, G_, cols], g_sq[:], 1.0, ALU.subtract, gate[I_][:], ALU.mult)
@@ -206,7 +208,7 @@ def tile_lstmcell_t_v_kernel(
                     stt(through[:], through[:], 1.0, ALU.subtract, dcn[:, cols], ALU.mult)
                     stt(
                         fac[:, O_, cols], tanh_c[:], gain_neg[:, O_ : O_ + 1], ALU.mult, fac[:, O_, cols], ALU.mult,
-                        parts3[:, O_, j : j + 1],
+                        mean_parts_v[:, 1, j : j + 1],
                     )
                     stt(dcn[:, cols], through[:], -1.0, ALU.mult, g0[:], ALU.add, parts2[:, 0, j : j + 1])
                     junk = p23.tile([P, CH], F32)
@@ -217,38 +219,43 @@ def tile_lstmcell_t_v_kernel(
                 nc.vector.tensor_tensor(out=lin2[:], in0=tot2[:], in1=coef2[:], op=ALU.mult)
                 stt(c_lin[:], lin2[:, 1:2], mean_neg[:, 0:1], ALU.mult, lin2[:, 0:1], ALU.add)
 
-                for j in range(NCH):
+                def dv_and_products(j):
                     cols = slice(j * CH, (j + 1) * CH)
-                    xt = {}
-                    for kind in (O_, F_, I_, G_):
-                        xt[kind] = psum.tile([P, CH], F32, tag="wide", name="xt%d" % kind)
-                        transpose_slices(
-                            xt[kind], lambda s: xhat[:, j * SL + s, kind * HID : (kind + 1) * HID], ident_f
-                        )
                     dv = p23.tile([P, CH], F32)
                     nc.scalar.activation(
                         out=dv[:], in_=cell[:, cols], func=ACT.Identity, bias=c_lin[:, 0:1], scale=lin2[:, 1:2]
                     )
-
-                    def times_xhat(kind):
-                        junk = p23.tile([P, CH], F32)
-                        stt(
-                            junk[:], fac[:, kind, cols], 1.0, ALU.mult, xt[kind][:], ALU.mult,
-                            parts3[:, KINDS + kind, j : j + 1],
-                        )
-
-                    times_xhat(O_)
                     stt(dv[:], dcn[:, cols], a_tc[:, 0:1], ALU.mult, dv[:], ALU.add)
-                    for kind in (F_, I_, G_):
-                        stt(
-                            fac[:, kind, cols], dv[:], gain_neg[:, kind : kind + 1], ALU.mult, fac[:, kind, cols],
-                            ALU.mult, parts3[:, kind, j : j + 1],
+                    stt(
+                        fac[:, F_, cols], dv[:], gain_neg[:, F_ : F_ + 1], ALU.mult, fac[:, F_, cols], ALU.mult,
+                        mean_parts_v[:, 0, j : j + 1],
+                    )
+                    for n, kind in enumerate((I_, G_)):
+                        raw = p23.tile([P, CH], F32, name="raw%d" % kind)
+                        nc.gpsimd.tensor_tensor(out=raw[:], in0=dv[:], in1=fac[:, kind, cols], op=ALU.mult)
+                        nc.scalar.activation(
+                            out=fac[:, kind, cols], in_=raw[:], func=ACT.Identity,
+                            scale=gain_neg[:, kind : kind + 1], accum_out=mean_parts_s[:, n, j : j + 1],
                         )
-                    for kind in (F_, I_, G_):
-                        times_xhat(kind)
+
+                def sums_with_xhat(j):
+                    cols = slice(j * CH, (j + 1) * CH)
+                    for kind in (O_, F_, I_, G_):
+                        xt = psum.tile([P, CH], F32, tag="wide")
+                        transpose_slices(xt, lambda s: xhat[:, j * SL + s, kind * HID : (kind + 1) * HID], ident_f)
+                        junk = p23.tile([P, CH], F32)
+                        stt(junk[:], fac[:, kind, cols], 1.0, ALU.mult, xt[:], ALU.mult, corr_parts[:, kind, j : j + 1])
+
+                dv_and_products(0)
+                for j in range(NCH):
+                    if j + 1 < NCH:
+                        dv_and_products(j + 1)
+                    sums_with_xhat(j)
 
                 tot3 = p23.tile([P, 2 * KINDS], F32)
-                nc.vector.reduce_sum(out=tot3[:], in_=parts3[:], axis=AX.X)
+                nc.vector.reduce_sum(out=tot3[:, 0:KINDS:2], in_=mean_parts_v[:], axis=AX.X)
+                nc.vector.reduce_sum(out=tot3[:, 1:KINDS:2], in_=mean_parts_s[:], axis=AX.X)
+                nc.vector.reduce_sum(out=tot3[:, KINDS : 2 * KINDS], in_=corr_parts[:], axis=AX.X)
                 nc.vector.tensor_scalar_mul(out=neg3[:], in0=tot3[:], scalar1=-1.0 / BATCH)
 
         with tc.tile_pool(name="p4", bufs=2) as p4:

@@ -25,6 +25,7 @@ CH = SL * P
 NCH = ROWS // SL
 EPS = 1e-5
 F_, I_, O_, G_ = 0, 1, 2, 3
+PINNED = {mybir.EngineType.DVE, mybir.EngineType.Pool}
 
 FLOPS = 2 * BATCH * GATES * WIDTH
 BYTES = 4 * 3 * BATCH * GATES + 2 * 3 * BATCH * HID + 2 * GATES * WIDTH + 6 * GATES + 4 * HID
@@ -134,9 +135,10 @@ def tile_lstmcell_t_v_kernel(
                     nc.scalar.activation(out=g_sq[:], in_=gate[G_][:], func=ACT.Square)
 
                     nc.vector.tensor_tensor(out=fac[:, F_, cols], in0=gate[F_][:], in1=cg[:, 0, :], op=ALU.mult)
-                    nc.gpsimd.tensor_tensor(out=fac[:, I_, cols], in0=gate[I_][:], in1=gate[G_][:], op=ALU.mult)
+                    ig = p1.tile([P, CH], F32, bufs=1)
+                    nc.gpsimd.tensor_tensor(out=ig[:], in0=gate[I_][:], in1=gate[G_][:], op=ALU.mult)
                     nc.vector.tensor_tensor(out=dcn[:, cols], in0=gate[O_][:], in1=cg[:, 1, :], op=ALU.mult)
-                    stt(cell[:, cols], fac[:, F_, cols], 1.0, ALU.mult, fac[:, I_, cols], ALU.add, sum_v[:, j : j + 1])
+                    stt(cell[:, cols], fac[:, F_, cols], 1.0, ALU.mult, ig[:], ALU.add, sum_v[:, j : j + 1])
                     nc.vector.tensor_scalar_mul(
                         out=chunk_mean_neg[:, j : j + 1], in0=sum_v[:, j : j + 1], scalar1=-1.0 / CH
                     )
@@ -145,20 +147,21 @@ def tile_lstmcell_t_v_kernel(
                         out=sq_junk[:], in_=cell[:, cols], func=ACT.Square,
                         bias=chunk_mean_neg[:, j : j + 1], scale=1.0, accum_out=sq_parts[:, j : j + 1],
                     )
-                    acts[j] = (gate, g_sq)
+                    acts[j] = (gate, g_sq, ig)
 
                 def gate_factors(j):
                     cols = slice(j * CH, (j + 1) * CH)
-                    gate, g_sq = acts[j]
+                    gate, g_sq, ig = acts[j]
                     stt(fac[:, F_, cols], gate[F_][:], 1.0, ALU.subtract, fac[:, F_, cols], ALU.mult)
-                    stt(fac[:, I_, cols], gate[I_][:], 1.0, ALU.subtract, fac[:, I_, cols], ALU.mult)
                     stt(fac[:, G_, cols], g_sq[:], 1.0, ALU.subtract, gate[I_][:], ALU.mult)
                     stt(fac[:, O_, cols], gate[O_][:], 1.0, ALU.subtract, dcn[:, cols], ALU.mult)
+                    stt(fac[:, I_, cols], gate[I_][:], 1.0, ALU.subtract, ig[:], ALU.mult)
 
-                for j in range(NCH):
-                    cell_value(j)
-                    if j < NCH - 1:
-                        gate_factors(j)
+                with tc.manual_schedule(engines=PINNED):
+                    for j in range(NCH):
+                        cell_value(j)
+                        if j < NCH - 1:
+                            gate_factors(j)
 
                 nc.sync.dma_start(out=g0_nat[:], in_=grad_v[:, 0, :, :])
                 nc.sync.dma_start(out=w_nat[:], in_=w_ih.rearrange("(t p) i -> p t i", p=P))
@@ -219,6 +222,8 @@ def tile_lstmcell_t_v_kernel(
                 nc.vector.tensor_tensor(out=lin2[:], in0=tot2[:], in1=coef2[:], op=ALU.mult)
                 stt(c_lin[:], lin2[:, 1:2], mean_neg[:, 0:1], ALU.mult, lin2[:, 0:1], ALU.add)
 
+                dvs = {}
+
                 def dv_and_products(j):
                     cols = slice(j * CH, (j + 1) * CH)
                     dv = p23.tile([P, CH], F32)
@@ -226,10 +231,7 @@ def tile_lstmcell_t_v_kernel(
                         out=dv[:], in_=cell[:, cols], func=ACT.Identity, bias=c_lin[:, 0:1], scale=lin2[:, 1:2]
                     )
                     stt(dv[:], dcn[:, cols], a_tc[:, 0:1], ALU.mult, dv[:], ALU.add)
-                    stt(
-                        fac[:, F_, cols], dv[:], gain_neg[:, F_ : F_ + 1], ALU.mult, fac[:, F_, cols], ALU.mult,
-                        mean_parts_v[:, 0, j : j + 1],
-                    )
+                    dvs[j] = dv
                     for n, kind in enumerate((I_, G_)):
                         raw = p23.tile([P, CH], F32, name="raw%d" % kind)
                         nc.gpsimd.tensor_tensor(out=raw[:], in0=dv[:], in1=fac[:, kind, cols], op=ALU.mult)
@@ -237,6 +239,13 @@ def tile_lstmcell_t_v_kernel(
                             out=fac[:, kind, cols], in_=raw[:], func=ACT.Identity,
                             scale=gain_neg[:, kind : kind + 1], accum_out=mean_parts_s[:, n, j : j + 1],
                         )
+
+                def forget_product(j):
+                    cols = slice(j * CH, (j + 1) * CH)
+                    stt(
+                        fac[:, F_, cols], dvs[j][:], gain_neg[:, F_ : F_ + 1], ALU.mult, fac[:, F_, cols], ALU.mult,
+                        mean_parts_v[:, 0, j : j + 1],
+                    )
 
                 def sums_with_xhat(j):
                     cols = slice(j * CH, (j + 1) * CH)
@@ -246,11 +255,15 @@ def tile_lstmcell_t_v_kernel(
                         junk = p23.tile([P, CH], F32)
                         stt(junk[:], fac[:, kind, cols], 1.0, ALU.mult, xt[:], ALU.mult, corr_parts[:, kind, j : j + 1])
 
-                dv_and_products(0)
-                for j in range(NCH):
-                    if j + 1 < NCH:
-                        dv_and_products(j + 1)
-                    sums_with_xhat(j)
+                with tc.manual_schedule(engines=PINNED):
+                    dv_and_products(0)
+                    forget_product(0)
+                    for j in range(NCH):
+                        if j + 1 < NCH:
+                            dv_and_products(j + 1)
+                        sums_with_xhat(j)
+                        if j + 1 < NCH:
+                            forget_product(j + 1)
 
                 tot3 = p23.tile([P, 2 * KINDS], F32)
                 nc.vector.reduce_sum(out=tot3[:, 0:KINDS:2], in_=mean_parts_v[:], axis=AX.X)

@@ -83,17 +83,19 @@ def tile_lstmcell_t_v_kernel(
         stt(gain_neg[:], vecs[:, 0:KINDS], -1.0, ALU.mult, cols_f[:, 0:KINDS], ALU.mult)
 
         fac = keep.tile([P, KINDS, BATCH], F32)
-        xhat = keep.tile([P, ROWS, GATES], F32)
+        xh_lo = keep.tile([P, ROWS // 2, GATES], F32)
+        cell = keep.tile([P, BATCH], F32)
+        dcn = keep.tile([P, BATCH], F32)
+        g0_nat = keep.tile([P, ROWS, HID], BF16)
         w_nat = keep.tile([P, KINDS, WIDTH], BF16)
+        w_grouped = keep.tile([P, WIDTH, KINDS], BF16, align_bytes=64)
         w_codes = keep.tile([P, WIDTH], U32, align_bytes=64)
         w_scales = keep.tile([P, WIDTH], U8, align_bytes=64)
         sum_v = keep.tile([P, NCH], F32)
-        chunk_mean_neg = keep.tile([P, NCH], F32)
         sq_parts = keep.tile([P, NCH], F32)
         parts2 = keep.tile([P, 2, NCH], F32)
-        mean_parts_v = keep.tile([P, 2, NCH], F32)
-        mean_parts_s = keep.tile([P, 2, NCH], F32)
-        corr_parts = keep.tile([P, KINDS, NCH], F32)
+        parts3 = keep.tile([P, 2 * KINDS, NCH], F32)
+        shift_neg = keep.tile([P, 1], F32)
         mean_neg = keep.tile([P, 1], F32)
         a_tc = keep.tile([P, 1], F32)
         b_tc = keep.tile([P, 1], F32)
@@ -101,198 +103,272 @@ def tile_lstmcell_t_v_kernel(
         lin2 = keep.tile([P, 2], F32)
         c_lin = keep.tile([P, 1], F32)
         neg3 = keep.tile([P, 2 * KINDS], F32)
+        small = stack.enter_context(tc.tile_pool(name="small", bufs=1))
+        p2 = stack.enter_context(tc.tile_pool(name="p2", bufs=2))
+        stack.enter_context(tc.manual_schedule(engines=PINNED))
 
+        def columns(j):
+            return slice(j * CH, (j + 1) * CH)
 
-        with tc.tile_pool(name="mid", bufs=1) as mid:
-            cell = mid.tile([P, BATCH], F32)
-            dcn = mid.tile([P, BATCH], F32)
-            g0_nat = mid.tile([P, ROWS, HID], BF16)
+        def quantise_weights_copy():
+            nc.vector.tensor_copy(
+                out=w_grouped[:].rearrange("p (c i) t -> p c t i", i=4),
+                in_=w_nat[:].rearrange("p t (c i) -> p c t i", i=4),
+            )
 
-            with tc.tile_pool(name="p1", bufs=2) as p1:
-                acts = {}
+        def quantise_weights():
+            nc.vector.quantize_mx(
+                out=w_codes[:].bitcast(E4M3X4), scales=w_scales[:], in_=w_grouped[:].rearrange("p i t -> p (i t)")
+            )
 
-                def cell_value(j):
-                    sl = slice(j * SL, (j + 1) * SL)
-                    cols = slice(j * CH, (j + 1) * CH)
-                    z_nat = p1.tile([P, SL, GATES], F32, bufs=3)
-                    nc.sync.dma_start(out=z_nat[:], in_=gates_v[:, sl, :])
-                    c_nat = p1.tile([P, SL, HID], BF16, bufs=3)
-                    nc.sync.dma_start(out=c_nat[:], in_=c_v[:, sl, :])
-                    g1_nat = p1.tile([P, SL, HID], BF16, bufs=3)
+        tanhs = {}
+        throughs = {}
+        g0s = {}
+
+        def tanh_and_square(j):
+            g0 = psum.tile([P, CH], BF16, tag="rest")
+            transpose_slices(g0, lambda s: g0_nat[:, j * SL + s, :], ident_b)
+            tanh_c = p2.tile([P, CH], F32)
+            nc.scalar.activation(
+                out=tanh_c[:], in_=cell[:, columns(j)], func=ACT.Tanh, bias=b_tc[:, 0:1], scale=a_tc[:, 0:1]
+            )
+            through = p2.tile([P, CH], F32)
+            nc.scalar.activation(out=through[:], in_=tanh_c[:], func=ACT.Square)
+            tanhs[j], throughs[j], g0s[j] = tanh_c, through, g0
+
+        def through_tanh(j):
+            stt(throughs[j][:], throughs[j][:], 1.0, ALU.subtract, dcn[:, columns(j)], ALU.mult)
+
+        def out_gate_and_dcn(j):
+            cols = columns(j)
+            stt(
+                fac[:, O_, cols], tanhs[j][:], gain_neg[:, O_ : O_ + 1], ALU.mult, fac[:, O_, cols], ALU.mult,
+                parts3[:, O_, j : j + 1],
+            )
+            stt(dcn[:, cols], throughs[j][:], -1.0, ALU.mult, g0s[j][:], ALU.add, parts2[:, 0, j : j + 1])
+
+        def dcn_with_cell(j):
+            cols = columns(j)
+            junk = p2.tile([P, CH], BF16)
+            stt(junk[:], cell[:, cols], mean_neg[:, 0:1], ALU.add, dcn[:, cols], ALU.mult, parts2[:, 1, j : j + 1])
+
+        with tc.tile_pool(name="p1", bufs=2) as p1:
+            acts = {}
+
+            def load_and_activate(j):
+                sl = slice(j * SL, (j + 1) * SL)
+                z_nat = p1.tile([P, SL, GATES], F32, bufs=3)
+                c_nat = p1.tile([P, SL, HID], BF16, bufs=3)
+                g1_nat = p1.tile([P, SL, HID], BF16, bufs=3)
+                if j == 0:
+                    for kind in (F_, I_, G_, O_):
+                        ks = slice(kind * HID, (kind + 1) * HID)
+                        nc.sync.dma_start(out=z_nat[:, :, ks], in_=gates_v[:, sl, ks])
+                        if kind == F_:
+                            nc.sync.dma_start(out=c_nat[:], in_=c_v[:, sl, :])
                     nc.sync.dma_start(out=g1_nat[:], in_=grad_v[:, 1, sl, :])
+                else:
+                    nc.sync.dma_start(out=z_nat[:], in_=gates_v[:, sl, :])
+                    nc.sync.dma_start(out=c_nat[:], in_=c_v[:, sl, :])
+                    nc.sync.dma_start(out=g1_nat[:], in_=grad_v[:, 1, sl, :])
+                gate = {}
+                for kind in (F_, I_, G_, O_):
+                    z = psum.tile([P, CH], F32, tag="wide")
+                    transpose_slices(z, lambda s: z_nat[:, s, kind * HID : (kind + 1) * HID], ident_f)
+                    gate[kind] = p1.tile([P, CH], F32, name="gate%d" % kind)
+                    func = ACT.Tanh if kind == G_ else ACT.Sigmoid
+                    nc.scalar.activation(out=gate[kind][:], in_=z[:], func=func)
+                cg = psum.tile([P, 2, CH], BF16, tag="rest")
+                transpose_slices(cg[:, 0, :], lambda s: c_nat[:, s, :], ident_b)
+                transpose_slices(cg[:, 1, :], lambda s: g1_nat[:, s, :], ident_b)
+                f_sq = p1.tile([P, CH], F32)
+                nc.scalar.activation(out=f_sq[:], in_=gate[F_][:], func=ACT.Square, bias=neg_half[:, 0:1])
+                g_sq = p1.tile([P, CH], F32)
+                nc.scalar.activation(out=g_sq[:], in_=gate[G_][:], func=ACT.Square)
+                ig = p1.tile([P, CH], F32, bufs=1)
+                nc.gpsimd.tensor_tensor(out=ig[:], in0=gate[I_][:], in1=gate[G_][:], op=ALU.mult)
+                acts[j] = (gate, f_sq, g_sq, ig, cg)
 
-                    cg = psum.tile([P, 2, CH], BF16, tag="rest")
-                    transpose_slices(cg[:, 0, :], lambda s: c_nat[:, s, :], ident_b)
-                    transpose_slices(cg[:, 1, :], lambda s: g1_nat[:, s, :], ident_b)
-                    gate = {}
-                    for kind in (F_, O_, I_, G_):
-                        z = psum.tile([P, CH], F32, tag="wide")
-                        transpose_slices(z, lambda s: z_nat[:, s, kind * HID : (kind + 1) * HID], ident_f)
-                        gate[kind] = p1.tile([P, CH], F32, name="gate%d" % kind)
-                        func = ACT.Tanh if kind == G_ else ACT.Sigmoid
-                        nc.scalar.activation(out=gate[kind][:], in_=z[:], func=func)
-                    g_sq = p1.tile([P, CH], F32)
-                    nc.scalar.activation(out=g_sq[:], in_=gate[G_][:], func=ACT.Square)
+            def cell_value(j):
+                cols = columns(j)
+                gate, f_sq, g_sq, ig, cg = acts[j]
+                nc.vector.tensor_tensor(out=cell[:, cols], in0=gate[F_][:], in1=cg[:, 0, :], op=ALU.mult)
+                nc.vector.tensor_tensor(out=dcn[:, cols], in0=gate[O_][:], in1=cg[:, 1, :], op=ALU.mult)
+                stt(fac[:, F_, cols], f_sq[:], 0.25, ALU.subtract, cg[:, 0, :], ALU.mult)
+                stt(cell[:, cols], cell[:, cols], 1.0, ALU.mult, ig[:], ALU.add, sum_v[:, j : j + 1])
+                if j == 0:
+                    nc.vector.tensor_scalar_mul(out=shift_neg[:], in0=sum_v[:, 0:1], scalar1=-1.0 / CH)
+                sq_junk = p1.tile([P, CH], BF16)
+                nc.scalar.activation(
+                    out=sq_junk[:], in_=cell[:, cols], func=ACT.Square,
+                    bias=shift_neg[:, 0:1], scale=1.0, accum_out=sq_parts[:, j : j + 1],
+                )
 
-                    nc.vector.tensor_tensor(out=fac[:, F_, cols], in0=gate[F_][:], in1=cg[:, 0, :], op=ALU.mult)
-                    ig = p1.tile([P, CH], F32, bufs=1)
-                    nc.gpsimd.tensor_tensor(out=ig[:], in0=gate[I_][:], in1=gate[G_][:], op=ALU.mult)
-                    nc.vector.tensor_tensor(out=dcn[:, cols], in0=gate[O_][:], in1=cg[:, 1, :], op=ALU.mult)
-                    stt(cell[:, cols], fac[:, F_, cols], 1.0, ALU.mult, ig[:], ALU.add, sum_v[:, j : j + 1])
-                    nc.vector.tensor_scalar_mul(
-                        out=chunk_mean_neg[:, j : j + 1], in0=sum_v[:, j : j + 1], scalar1=-1.0 / CH
-                    )
-                    sq_junk = p1.tile([P, CH], BF16)
-                    nc.scalar.activation(
-                        out=sq_junk[:], in_=cell[:, cols], func=ACT.Square,
-                        bias=chunk_mean_neg[:, j : j + 1], scale=1.0, accum_out=sq_parts[:, j : j + 1],
-                    )
-                    acts[j] = (gate, g_sq, ig)
-
-                def gate_factors(j):
-                    cols = slice(j * CH, (j + 1) * CH)
-                    gate, g_sq, ig = acts[j]
-                    stt(fac[:, F_, cols], gate[F_][:], 1.0, ALU.subtract, fac[:, F_, cols], ALU.mult)
+            def factor(kind, j):
+                cols = columns(j)
+                gate, f_sq, g_sq, ig, cg = acts[j]
+                if kind == G_:
                     stt(fac[:, G_, cols], g_sq[:], 1.0, ALU.subtract, gate[I_][:], ALU.mult)
+                elif kind == O_:
                     stt(fac[:, O_, cols], gate[O_][:], 1.0, ALU.subtract, dcn[:, cols], ALU.mult)
+                else:
                     stt(fac[:, I_, cols], gate[I_][:], 1.0, ALU.subtract, ig[:], ALU.mult)
 
-                with tc.manual_schedule(engines=PINNED):
-                    for j in range(NCH):
-                        cell_value(j)
-                        if j < NCH - 1:
-                            gate_factors(j)
+            for j in range(NCH):
+                load_and_activate(j)
+                cell_value(j)
+                if j < NCH - 2:
+                    factor(G_, j)
+                    factor(O_, j)
+                if j < NCH - 1:
+                    factor(I_, j)
 
-                nc.sync.dma_start(out=g0_nat[:], in_=grad_v[:, 0, :, :])
-                nc.sync.dma_start(out=w_nat[:], in_=w_ih.rearrange("(t p) i -> p t i", p=P))
-                for j in range(NCH):
-                    sl = slice(j * SL, (j + 1) * SL)
-                    nc.sync.dma_start(out=xhat[:, sl, :], in_=xhat_v[:, sl, :])
+            nc.sync.dma_start(out=g0_nat[:], in_=grad_v[:, 0, :, :])
+            nc.sync.dma_start(out=w_nat[:], in_=w_ih.rearrange("(t p) i -> p t i", p=P))
+            for j in range(NCH // 2):
+                sl = slice(j * SL, (j + 1) * SL)
+                nc.sync.dma_start(out=xh_lo[:, sl, :], in_=xhat_v[:, sl, :])
 
-                tot_v = p1.tile([P, 1], F32)
-                nc.vector.reduce_sum(out=tot_v[:], in_=sum_v[:], axis=AX.X)
-                nc.vector.tensor_scalar_mul(out=mean_neg[:], in0=tot_v[:], scalar1=-1.0 / BATCH)
-                dev = p1.tile([P, NCH], F32)
-                nc.vector.tensor_scalar_sub(out=dev[:], in0=chunk_mean_neg[:], scalar1=mean_neg[:, 0:1])
-                dev_sq = p1.tile([P, NCH], F32)
-                between = p1.tile([P, 1], F32)
-                stt(dev_sq[:], dev[:], float(CH), ALU.mult, dev[:], ALU.mult, between[:])
-                within = p1.tile([P, 1], F32)
-                nc.vector.reduce_sum(out=within[:], in_=sq_parts[:], axis=AX.X)
-                spread = p1.tile([P, 1], F32)
-                nc.vector.tensor_tensor(out=spread[:], in0=between[:], in1=within[:], op=ALU.add)
-                var_eps = p1.tile([P, 1], F32)
-                nc.vector.tensor_scalar(
-                    out=var_eps[:], in0=spread[:], scalar1=1.0 / BATCH, scalar2=EPS, op0=ALU.mult, op1=ALU.add
+            tot_v = small.tile([P, 1], F32)
+            nc.vector.reduce_sum(out=tot_v[:], in_=sum_v[:], axis=AX.X)
+            nc.vector.tensor_scalar_mul(out=mean_neg[:], in0=tot_v[:], scalar1=-1.0 / BATCH)
+            off = small.tile([P, 1], F32)
+            nc.vector.tensor_tensor(out=off[:], in0=mean_neg[:], in1=shift_neg[:], op=ALU.subtract)
+            off_sq_neg = small.tile([P, 1], F32)
+            stt(off_sq_neg[:], off[:], -1.0, ALU.mult, off[:], ALU.mult)
+            factor(G_, NCH - 2)
+            factor(O_, NCH - 2)
+            within = small.tile([P, 1], F32)
+            nc.vector.reduce_sum(out=within[:], in_=sq_parts[:], axis=AX.X)
+            spread = small.tile([P, 1], F32)
+            nc.vector.tensor_scalar(
+                out=spread[:], in0=within[:], scalar1=1.0 / BATCH, scalar2=EPS, op0=ALU.mult, op1=ALU.add
+            )
+            var_eps = small.tile([P, 1], F32)
+            nc.vector.tensor_tensor(out=var_eps[:], in0=spread[:], in1=off_sq_neg[:], op=ALU.add)
+            rstd = small.tile([P, 1], F32)
+            nc.gpsimd.tensor_tensor(out=rstd[:], in0=var_eps[:], in1=neg_half[:], op=ALU.pow)
+            factor(G_, NCH - 1)
+            factor(O_, NCH - 1)
+            nc.vector.tensor_tensor(out=a_tc[:], in0=rstd[:], in1=gamma_c, op=ALU.mult)
+            stt(b_tc[:], mean_neg[:], a_tc[:, 0:1], ALU.mult, beta_c, ALU.add)
+            tanh_and_square(0)
+            factor(I_, NCH - 1)
+            rstd_sq = small.tile([P, 1], F32)
+            nc.vector.tensor_tensor(out=rstd_sq[:], in0=rstd[:], in1=rstd[:], op=ALU.mult)
+            nc.vector.tensor_scalar_mul(out=coef2[:, 0:1], in0=a_tc[:], scalar1=-1.0 / BATCH)
+            nc.vector.tensor_tensor(out=coef2[:, 1:2], in0=coef2[:, 0:1], in1=rstd_sq[:], op=ALU.mult)
+
+        late = stack.enter_context(tc.tile_pool(name="late", bufs=1, reuse_waits="tile"))
+        xh_hi = late.tile([P, ROWS // 2, GATES], F32)
+        for j in range(NCH // 2):
+            sl = slice(j * SL, (j + 1) * SL)
+            nc.sync.dma_start(out=xh_hi[:, sl, :], in_=xhat_v[:, ROWS // 2 + j * SL : ROWS // 2 + (j + 1) * SL, :])
+
+        def xhat_block(row, kind):
+            half = xh_lo if row < ROWS // 2 else xh_hi
+            return half[:, row % (ROWS // 2), kind * HID : (kind + 1) * HID]
+
+        def xhat_transposed(j, kind):
+            xt = psum.tile([P, CH], F32, tag="wide")
+            transpose_slices(xt, lambda s: xhat_block(j * SL + s, kind), ident_f)
+            return xt
+
+        through_tanh(0)
+        for j in range(NCH):
+            out_gate_and_dcn(j)
+            if j + 1 < NCH:
+                tanh_and_square(j + 1)
+                through_tanh(j + 1)
+            dcn_with_cell(j)
+
+        tot2 = small.tile([P, 2], F32)
+        nc.vector.reduce_sum(out=tot2[:], in_=parts2[:], axis=AX.X)
+        nc.vector.tensor_tensor(out=lin2[:], in0=tot2[:], in1=coef2[:], op=ALU.mult)
+        stt(c_lin[:], lin2[:, 1:2], mean_neg[:, 0:1], ALU.mult, lin2[:, 0:1], ALU.add)
+
+        with tc.tile_pool(name="p3", bufs=2, reuse_waits="tile") as p3:
+            dvs = {}
+
+            def dv_and_products(j):
+                cols = columns(j)
+                dv = p3.tile([P, CH], F32)
+                nc.scalar.activation(
+                    out=dv[:], in_=cell[:, cols], func=ACT.Identity, bias=c_lin[:, 0:1], scale=lin2[:, 1:2]
                 )
-                rstd = p1.tile([P, 1], F32)
-                nc.gpsimd.tensor_tensor(out=rstd[:], in0=var_eps[:], in1=neg_half[:], op=ALU.pow)
-                nc.vector.tensor_tensor(out=a_tc[:], in0=rstd[:], in1=gamma_c, op=ALU.mult)
-                stt(b_tc[:], mean_neg[:], a_tc[:, 0:1], ALU.mult, beta_c, ALU.add)
-
-                gate_factors(NCH - 1)
-
-                rstd_sq = p1.tile([P, 1], F32)
-                nc.vector.tensor_tensor(out=rstd_sq[:], in0=rstd[:], in1=rstd[:], op=ALU.mult)
-                nc.vector.tensor_scalar_mul(out=coef2[:, 0:1], in0=a_tc[:], scalar1=-1.0 / BATCH)
-                nc.vector.tensor_tensor(out=coef2[:, 1:2], in0=coef2[:, 0:1], in1=rstd_sq[:], op=ALU.mult)
-
-            with tc.tile_pool(name="p23", bufs=2, reuse_waits="tile") as p23:
-                for j in range(NCH):
-                    cols = slice(j * CH, (j + 1) * CH)
-                    g0 = psum.tile([P, CH], BF16, tag="rest")
-                    transpose_slices(g0, lambda s: g0_nat[:, j * SL + s, :], ident_b)
-                    tanh_c = p23.tile([P, CH], F32)
+                if j == 0:
+                    quantise_weights_copy()
+                    quantise_weights()
+                stt(dv[:], dcn[:, cols], a_tc[:, 0:1], ALU.mult, dv[:], ALU.add)
+                dvs[j] = dv
+                for kind in (I_, G_):
+                    raw = p3.tile([P, CH], F32, name="raw%d" % kind)
+                    nc.gpsimd.tensor_tensor(out=raw[:], in0=dv[:], in1=fac[:, kind, cols], op=ALU.mult)
                     nc.scalar.activation(
-                        out=tanh_c[:], in_=cell[:, cols], func=ACT.Tanh, bias=b_tc[:, 0:1], scale=a_tc[:, 0:1]
+                        out=fac[:, kind, cols], in_=raw[:], func=ACT.Identity,
+                        scale=gain_neg[:, kind : kind + 1], accum_out=parts3[:, kind, j : j + 1],
                     )
-                    through = p23.tile([P, CH], F32)
-                    nc.scalar.activation(out=through[:], in_=tanh_c[:], func=ACT.Square)
-                    stt(through[:], through[:], 1.0, ALU.subtract, dcn[:, cols], ALU.mult)
+
+            def forget_product(j):
+                cols = columns(j)
+                stt(
+                    fac[:, F_, cols], dvs[j][:], gain_neg[:, F_ : F_ + 1], ALU.mult, fac[:, F_, cols], ALU.mult,
+                    parts3[:, F_, j : j + 1],
+                )
+
+            def sums_with_xhat(j):
+                for kind in (O_, F_, I_, G_):
+                    xt = xhat_transposed(j, kind)
+                    junk = p2.tile([P, CH], BF16)
                     stt(
-                        fac[:, O_, cols], tanh_c[:], gain_neg[:, O_ : O_ + 1], ALU.mult, fac[:, O_, cols], ALU.mult,
-                        mean_parts_v[:, 1, j : j + 1],
-                    )
-                    stt(dcn[:, cols], through[:], -1.0, ALU.mult, g0[:], ALU.add, parts2[:, 0, j : j + 1])
-                    junk = p23.tile([P, CH], F32)
-                    stt(junk[:], cell[:, cols], mean_neg[:, 0:1], ALU.add, dcn[:, cols], ALU.mult, parts2[:, 1, j : j + 1])
-
-                tot2 = p23.tile([P, 2], F32)
-                nc.vector.reduce_sum(out=tot2[:], in_=parts2[:], axis=AX.X)
-                nc.vector.tensor_tensor(out=lin2[:], in0=tot2[:], in1=coef2[:], op=ALU.mult)
-                stt(c_lin[:], lin2[:, 1:2], mean_neg[:, 0:1], ALU.mult, lin2[:, 0:1], ALU.add)
-
-                dvs = {}
-
-                def dv_and_products(j):
-                    cols = slice(j * CH, (j + 1) * CH)
-                    dv = p23.tile([P, CH], F32)
-                    nc.scalar.activation(
-                        out=dv[:], in_=cell[:, cols], func=ACT.Identity, bias=c_lin[:, 0:1], scale=lin2[:, 1:2]
-                    )
-                    stt(dv[:], dcn[:, cols], a_tc[:, 0:1], ALU.mult, dv[:], ALU.add)
-                    dvs[j] = dv
-                    for n, kind in enumerate((I_, G_)):
-                        raw = p23.tile([P, CH], F32, name="raw%d" % kind)
-                        nc.gpsimd.tensor_tensor(out=raw[:], in0=dv[:], in1=fac[:, kind, cols], op=ALU.mult)
-                        nc.scalar.activation(
-                            out=fac[:, kind, cols], in_=raw[:], func=ACT.Identity,
-                            scale=gain_neg[:, kind : kind + 1], accum_out=mean_parts_s[:, n, j : j + 1],
-                        )
-
-                def forget_product(j):
-                    cols = slice(j * CH, (j + 1) * CH)
-                    stt(
-                        fac[:, F_, cols], dvs[j][:], gain_neg[:, F_ : F_ + 1], ALU.mult, fac[:, F_, cols], ALU.mult,
-                        mean_parts_v[:, 0, j : j + 1],
+                        junk[:], fac[:, kind, columns(j)], 1.0, ALU.mult, xt[:], ALU.mult,
+                        parts3[:, KINDS + kind, j : j + 1],
                     )
 
-                def sums_with_xhat(j):
-                    cols = slice(j * CH, (j + 1) * CH)
-                    for kind in (O_, F_, I_, G_):
-                        xt = psum.tile([P, CH], F32, tag="wide")
-                        transpose_slices(xt, lambda s: xhat[:, j * SL + s, kind * HID : (kind + 1) * HID], ident_f)
-                        junk = p23.tile([P, CH], F32)
-                        stt(junk[:], fac[:, kind, cols], 1.0, ALU.mult, xt[:], ALU.mult, corr_parts[:, kind, j : j + 1])
+            dv_and_products(0)
+            forget_product(0)
+            for j in range(NCH):
+                if j + 1 < NCH:
+                    dv_and_products(j + 1)
+                sums_with_xhat(j)
+                if j + 1 < NCH:
+                    forget_product(j + 1)
 
-                with tc.manual_schedule(engines=PINNED):
-                    dv_and_products(0)
-                    forget_product(0)
-                    for j in range(NCH):
-                        if j + 1 < NCH:
-                            dv_and_products(j + 1)
-                        sums_with_xhat(j)
-                        if j + 1 < NCH:
-                            forget_product(j + 1)
+            tot3 = small.tile([P, 2 * KINDS], F32)
+            nc.vector.reduce_sum(out=tot3[:], in_=parts3[:], axis=AX.X)
+            nc.vector.tensor_scalar_mul(out=neg3[:], in0=tot3[:], scalar1=-1.0 / BATCH)
 
-                tot3 = p23.tile([P, 2 * KINDS], F32)
-                nc.vector.reduce_sum(out=tot3[:, 0:KINDS:2], in_=mean_parts_v[:], axis=AX.X)
-                nc.vector.reduce_sum(out=tot3[:, 1:KINDS:2], in_=mean_parts_s[:], axis=AX.X)
-                nc.vector.reduce_sum(out=tot3[:, KINDS : 2 * KINDS], in_=corr_parts[:], axis=AX.X)
-                nc.vector.tensor_scalar_mul(out=neg3[:], in0=tot3[:], scalar1=-1.0 / BATCH)
-
-        with tc.tile_pool(name="p4", bufs=2) as p4:
-            shifts = {}
+        with tc.tile_pool(name="p4", bufs=2, reuse_waits="tile") as p4:
             sums = {}
 
+            def shift_buffer(j):
+                half = (j % 2) * KINDS * CH
+                return dcn[:, half : half + KINDS * CH].rearrange("p (t b) -> p t b", t=KINDS)
+
+            def result_buffer(j):
+                half = (j % 2) * SL * WIDTH
+                return cell[:, half : half + SL * WIDTH].rearrange("p (s i) -> p s i", s=SL)
+
             def shift_terms(j):
-                shift = p4.tile([P, KINDS, CH], F32)
                 for kind in range(KINDS):
-                    xt = psum.tile([P, CH], F32, tag="wide")
-                    transpose_slices(xt, lambda s: xhat[:, j * SL + s, kind * HID : (kind + 1) * HID], ident_f)
-                    nc.scalar.activation(
-                        out=shift[:, kind, :], in_=xt[:], func=ACT.Identity,
-                        bias=neg3[:, kind : kind + 1], scale=neg3[:, KINDS + kind : KINDS + kind + 1],
-                    )
-                shifts[j] = shift
+                    xt = xhat_transposed(j, kind)
+                    if j == 0 and kind >= 2:
+                        nc.vector.tensor_scalar(
+                            out=shift_buffer(j)[:, kind, :], in0=xt[:], scalar1=neg3[:, KINDS + kind : KINDS + kind + 1],
+                            scalar2=neg3[:, kind : kind + 1], op0=ALU.mult, op1=ALU.add,
+                        )
+                    else:
+                        nc.scalar.activation(
+                            out=shift_buffer(j)[:, kind, :], in_=xt[:], func=ACT.Identity,
+                            bias=neg3[:, kind : kind + 1], scale=neg3[:, KINDS + kind : KINDS + kind + 1],
+                        )
 
             def add_and_round(j):
-                cols = slice(j * CH, (j + 1) * CH)
                 da = p4.tile([P, CH, KINDS], BF16, align_bytes=64)
                 nc.vector.tensor_tensor(
                     out=da[:].rearrange("p (c i) t -> p c t i", i=4),
-                    in0=fac[:, :, cols].rearrange("p t (c i) -> p c t i", i=4),
-                    in1=shifts[j][:].rearrange("p t (c i) -> p c t i", i=4),
+                    in0=fac[:, :, columns(j)].rearrange("p t (c i) -> p c t i", i=4),
+                    in1=shift_buffer(j).rearrange("p t (c i) -> p c t i", i=4),
                     op=ALU.add,
                 )
                 return da
@@ -319,23 +395,18 @@ def tile_lstmcell_t_v_kernel(
                     sums[j].append(acc)
 
             def store(j):
-                result = p4.tile([P, SL, WIDTH], F32, bufs=3)
+                result = result_buffer(j)
                 for s in range(SL):
                     if s % 2 == 0:
                         nc.scalar.copy(out=result[:, s, :], in_=sums[j][s][:])
                     else:
                         nc.vector.tensor_copy(out=result[:, s, :], in_=sums[j][s][:])
-                nc.sync.dma_start(out=out_v[:, j * SL : (j + 1) * SL, :], in_=result[:])
+                    if j == NCH - 1:
+                        nc.sync.dma_start(out=out_v[:, j * SL + s, :], in_=result[:, s, :])
+                if j < NCH - 1:
+                    nc.sync.dma_start(out=out_v[:, j * SL : (j + 1) * SL, :], in_=result)
 
             shift_terms(0)
-            w_grouped = p4.tile([P, WIDTH, KINDS], BF16, align_bytes=64, bufs=1)
-            nc.vector.tensor_copy(
-                out=w_grouped[:].rearrange("p (c i) t -> p c t i", i=4),
-                in_=w_nat[:].rearrange("p t (c i) -> p c t i", i=4),
-            )
-            nc.vector.quantize_mx(
-                out=w_codes[:].bitcast(E4M3X4), scales=w_scales[:], in_=w_grouped[:].rearrange("p i t -> p (i t)")
-            )
             for j in range(NCH + 1):
                 if j + 1 < NCH:
                     shift_terms(j + 1)

@@ -25,6 +25,8 @@ CH = SL * P
 NCH = ROWS // SL
 EPS = 1e-5
 F_, I_, O_, G_ = 0, 1, 2, 3
+LATE_FACTORS = 3
+LATE_OUT = 5
 PINNED = {mybir.EngineType.DVE, mybir.EngineType.Pool}
 
 FLOPS = 2 * BATCH * GATES * WIDTH
@@ -128,7 +130,7 @@ def tile_lstmcell_t_v_kernel(
         def tanh_and_square(j):
             g0 = psum.tile([P, CH], BF16, tag="rest")
             transpose_slices(g0, lambda s: g0_nat[:, j * SL + s, :], ident_b)
-            tanh_c = p2.tile([P, CH], F32)
+            tanh_c = p2.tile([P, CH], F32, bufs=LATE_OUT + 1)
             nc.scalar.activation(
                 out=tanh_c[:], in_=cell[:, columns(j)], func=ACT.Tanh, bias=b_tc[:, 0:1], scale=a_tc[:, 0:1]
             )
@@ -139,13 +141,15 @@ def tile_lstmcell_t_v_kernel(
         def through_tanh(j):
             stt(throughs[j][:], throughs[j][:], 1.0, ALU.subtract, dcn[:, columns(j)], ALU.mult)
 
-        def out_gate_and_dcn(j):
+        def out_gate(j):
             cols = columns(j)
             stt(
                 fac[:, O_, cols], tanhs[j][:], gain_neg[:, O_ : O_ + 1], ALU.mult, fac[:, O_, cols], ALU.mult,
                 parts3[:, O_, j : j + 1],
             )
-            stt(dcn[:, cols], throughs[j][:], -1.0, ALU.mult, g0s[j][:], ALU.add, parts2[:, 0, j : j + 1])
+
+        def dcn_value(j):
+            stt(dcn[:, columns(j)], throughs[j][:], -1.0, ALU.mult, g0s[j][:], ALU.add, parts2[:, 0, j : j + 1])
 
         def dcn_with_cell(j):
             cols = columns(j)
@@ -175,7 +179,7 @@ def tile_lstmcell_t_v_kernel(
                 for kind in (F_, I_, G_, O_):
                     z = psum.tile([P, CH], F32, tag="wide")
                     transpose_slices(z, lambda s: z_nat[:, s, kind * HID : (kind + 1) * HID], ident_f)
-                    gate[kind] = p1.tile([P, CH], F32, name="gate%d" % kind)
+                    gate[kind] = p1.tile([P, CH], F32, name="gate%d" % kind, bufs=LATE_FACTORS)
                     func = ACT.Tanh if kind == G_ else ACT.Sigmoid
                     nc.scalar.activation(out=gate[kind][:], in_=z[:], func=func)
                 cg = psum.tile([P, 2, CH], BF16, tag="rest")
@@ -183,18 +187,22 @@ def tile_lstmcell_t_v_kernel(
                 transpose_slices(cg[:, 1, :], lambda s: g1_nat[:, s, :], ident_b)
                 f_sq = p1.tile([P, CH], F32)
                 nc.scalar.activation(out=f_sq[:], in_=gate[F_][:], func=ACT.Square, bias=neg_half[:, 0:1])
-                g_sq = p1.tile([P, CH], F32)
+                g_sq = p1.tile([P, CH], F32, bufs=LATE_FACTORS)
                 nc.scalar.activation(out=g_sq[:], in_=gate[G_][:], func=ACT.Square)
                 ig = p1.tile([P, CH], F32, bufs=1)
                 nc.gpsimd.tensor_tensor(out=ig[:], in0=gate[I_][:], in1=gate[G_][:], op=ALU.mult)
                 acts[j] = (gate, f_sq, g_sq, ig, cg)
 
-            def cell_value(j):
+            def psum_products(j):
                 cols = columns(j)
                 gate, f_sq, g_sq, ig, cg = acts[j]
                 nc.vector.tensor_tensor(out=cell[:, cols], in0=gate[F_][:], in1=cg[:, 0, :], op=ALU.mult)
                 nc.vector.tensor_tensor(out=dcn[:, cols], in0=gate[O_][:], in1=cg[:, 1, :], op=ALU.mult)
                 stt(fac[:, F_, cols], f_sq[:], 0.25, ALU.subtract, cg[:, 0, :], ALU.mult)
+
+            def cell_sum(j):
+                cols = columns(j)
+                ig = acts[j][3]
                 stt(cell[:, cols], cell[:, cols], 1.0, ALU.mult, ig[:], ALU.add, sum_v[:, j : j + 1])
                 if j == 0:
                     nc.vector.tensor_scalar_mul(out=shift_neg[:], in0=sum_v[:, 0:1], scalar1=-1.0 / CH)
@@ -214,14 +222,25 @@ def tile_lstmcell_t_v_kernel(
                 else:
                     stt(fac[:, I_, cols], gate[I_][:], 1.0, ALU.subtract, ig[:], ALU.mult)
 
-            for j in range(NCH):
+            last = NCH - 1
+            for j in range(last):
                 load_and_activate(j)
-                cell_value(j)
-                if j < NCH - 2:
+                psum_products(j)
+                cell_sum(j)
+                if j < NCH - LATE_FACTORS:
                     factor(G_, j)
                     factor(O_, j)
-                if j < NCH - 1:
-                    factor(I_, j)
+                factor(I_, j)
+
+            sum_early = small.tile([P, 1], F32)
+            nc.vector.reduce_sum(out=sum_early[:], in_=sum_v[:, 0:last], axis=AX.X)
+            load_and_activate(last)
+            psum_products(last)
+            dev_early = small.tile([P, 1], F32)
+            stt(dev_early[:], shift_neg[:], float(BATCH), ALU.mult, sum_early[:], ALU.add)
+            sq_early = small.tile([P, 1], F32)
+            nc.vector.reduce_sum(out=sq_early[:], in_=sq_parts[:, 0:last], axis=AX.X)
+            cell_sum(last)
 
             nc.sync.dma_start(out=g0_nat[:], in_=grad_v[:, 0, :, :])
             nc.sync.dma_start(out=w_nat[:], in_=w_ih.rearrange("(t p) i -> p t i", p=P))
@@ -229,34 +248,36 @@ def tile_lstmcell_t_v_kernel(
                 sl = slice(j * SL, (j + 1) * SL)
                 nc.sync.dma_start(out=xh_lo[:, sl, :], in_=xhat_v[:, sl, :])
 
-            tot_v = small.tile([P, 1], F32)
-            nc.vector.reduce_sum(out=tot_v[:], in_=sum_v[:], axis=AX.X)
-            nc.vector.tensor_scalar_mul(out=mean_neg[:], in0=tot_v[:], scalar1=-1.0 / BATCH)
-            off = small.tile([P, 1], F32)
-            nc.vector.tensor_tensor(out=off[:], in0=mean_neg[:], in1=shift_neg[:], op=ALU.subtract)
-            off_sq_neg = small.tile([P, 1], F32)
-            stt(off_sq_neg[:], off[:], -1.0, ALU.mult, off[:], ALU.mult)
-            factor(G_, NCH - 2)
-            factor(O_, NCH - 2)
-            within = small.tile([P, 1], F32)
-            nc.vector.reduce_sum(out=within[:], in_=sq_parts[:], axis=AX.X)
-            spread = small.tile([P, 1], F32)
+            spread_early = small.tile([P, 1], F32)
             nc.vector.tensor_scalar(
-                out=spread[:], in0=within[:], scalar1=1.0 / BATCH, scalar2=EPS, op0=ALU.mult, op1=ALU.add
+                out=spread_early[:], in0=sq_early[:], scalar1=1.0 / BATCH, scalar2=EPS, op0=ALU.mult, op1=ALU.add
             )
+            factor(G_, last - 2)
+            dev = small.tile([P, 1], F32)
+            nc.vector.tensor_tensor(out=dev[:], in0=dev_early[:], in1=sum_v[:, last : last + 1], op=ALU.add)
+            factor(O_, last - 2)
+            dev_sq_neg = small.tile([P, 1], F32)
+            stt(dev_sq_neg[:], dev[:], -1.0 / (BATCH * BATCH), ALU.mult, dev[:], ALU.mult)
+            nc.vector.tensor_scalar(
+                out=mean_neg[:], in0=dev[:], scalar1=-1.0 / BATCH, scalar2=shift_neg[:, 0:1], op0=ALU.mult, op1=ALU.add
+            )
+            spread = small.tile([P, 1], F32)
+            stt(spread[:], sq_parts[:, last : last + 1], 1.0 / BATCH, ALU.mult, spread_early[:], ALU.add)
+            factor(G_, last - 1)
             var_eps = small.tile([P, 1], F32)
-            nc.vector.tensor_tensor(out=var_eps[:], in0=spread[:], in1=off_sq_neg[:], op=ALU.add)
+            nc.vector.tensor_tensor(out=var_eps[:], in0=spread[:], in1=dev_sq_neg[:], op=ALU.add)
             rstd = small.tile([P, 1], F32)
             nc.gpsimd.tensor_tensor(out=rstd[:], in0=var_eps[:], in1=neg_half[:], op=ALU.pow)
-            factor(G_, NCH - 1)
-            factor(O_, NCH - 1)
+            factor(O_, last - 1)
+            factor(G_, last)
             nc.vector.tensor_tensor(out=a_tc[:], in0=rstd[:], in1=gamma_c, op=ALU.mult)
+            factor(O_, last)
             stt(b_tc[:], mean_neg[:], a_tc[:, 0:1], ALU.mult, beta_c, ALU.add)
             tanh_and_square(0)
-            factor(I_, NCH - 1)
             rstd_sq = small.tile([P, 1], F32)
             nc.vector.tensor_tensor(out=rstd_sq[:], in0=rstd[:], in1=rstd[:], op=ALU.mult)
             nc.vector.tensor_scalar_mul(out=coef2[:, 0:1], in0=a_tc[:], scalar1=-1.0 / BATCH)
+            factor(I_, last)
             nc.vector.tensor_tensor(out=coef2[:, 1:2], in0=coef2[:, 0:1], in1=rstd_sq[:], op=ALU.mult)
 
         late = stack.enter_context(tc.tile_pool(name="late", bufs=1, reuse_waits="tile"))
@@ -276,15 +297,22 @@ def tile_lstmcell_t_v_kernel(
 
         through_tanh(0)
         for j in range(NCH):
-            out_gate_and_dcn(j)
+            if j < NCH - LATE_OUT:
+                out_gate(j)
+            dcn_value(j)
             if j + 1 < NCH:
                 tanh_and_square(j + 1)
                 through_tanh(j + 1)
+            else:
+                out_gate(NCH - 5)
             dcn_with_cell(j)
 
+        out_gate(NCH - 4)
         tot2 = small.tile([P, 2], F32)
         nc.vector.reduce_sum(out=tot2[:], in_=parts2[:], axis=AX.X)
+        out_gate(NCH - 3)
         nc.vector.tensor_tensor(out=lin2[:], in0=tot2[:], in1=coef2[:], op=ALU.mult)
+        out_gate(NCH - 2)
         stt(c_lin[:], lin2[:, 1:2], mean_neg[:, 0:1], ALU.mult, lin2[:, 0:1], ALU.add)
 
         with tc.tile_pool(name="p3", bufs=2, reuse_waits="tile") as p3:
@@ -297,8 +325,7 @@ def tile_lstmcell_t_v_kernel(
                     out=dv[:], in_=cell[:, cols], func=ACT.Identity, bias=c_lin[:, 0:1], scale=lin2[:, 1:2]
                 )
                 if j == 0:
-                    quantise_weights_copy()
-                    quantise_weights()
+                    out_gate(NCH - 1)
                 stt(dv[:], dcn[:, cols], a_tc[:, 0:1], ALU.mult, dv[:], ALU.add)
                 dvs[j] = dv
                 for kind in (I_, G_):
@@ -318,6 +345,8 @@ def tile_lstmcell_t_v_kernel(
 
             def sums_with_xhat(j):
                 for kind in (O_, F_, I_, G_):
+                    if j == NCH - 1 and kind == I_:
+                        quantise_weights_copy()
                     xt = xhat_transposed(j, kind)
                     junk = p2.tile([P, CH], BF16)
                     stt(
@@ -334,6 +363,7 @@ def tile_lstmcell_t_v_kernel(
                 if j + 1 < NCH:
                     forget_product(j + 1)
 
+            quantise_weights()
             tot3 = small.tile([P, 2 * KINDS], F32)
             nc.vector.reduce_sum(out=tot3[:], in_=parts3[:], axis=AX.X)
             nc.vector.tensor_scalar_mul(out=neg3[:], in0=tot3[:], scalar1=-1.0 / BATCH)
@@ -397,7 +427,7 @@ def tile_lstmcell_t_v_kernel(
             def store(j):
                 result = result_buffer(j)
                 for s in range(SL):
-                    if s % 2 == 0:
+                    if s % 2 == 0 or (s == 1 and j % 2 == 1):
                         nc.scalar.copy(out=result[:, s, :], in_=sums[j][s][:])
                     else:
                         nc.vector.tensor_copy(out=result[:, s, :], in_=sums[j][s][:])

@@ -73,7 +73,7 @@ def tile_lstmcell_t_v_kernel(
         nc.scalar.dma_start(out=rows_f[0:KINDS, :], in_=ih_rstd.rearrange("(t p) -> t p", p=P))
         nc.scalar.activation(out=warm[:], in_=neg_half[:], func=ACT.Sigmoid)
 
-        cols_b = psum.tile([P, P], BF16, tag="rest")
+        cols_b = psum.tile([P, P], BF16, tag="rest", bufs=3)
         nc.tensor.transpose(cols_b[:], rows_b[:], ident_b[:])
         cols_f = psum.tile([P, P], F32, tag="wide")
         nc.tensor.transpose(cols_f[:], rows_f[:], ident_f[:])
@@ -105,6 +105,7 @@ def tile_lstmcell_t_v_kernel(
         lin2 = keep.tile([P, 2], F32)
         c_lin = keep.tile([P, 1], F32)
         neg3 = keep.tile([P, 2 * KINDS], F32)
+        nc.vector.memset(parts3[:, KINDS + O_, :], 0.0)
         small = stack.enter_context(tc.tile_pool(name="small", bufs=1))
         p2 = stack.enter_context(tc.tile_pool(name="p2", bufs=2))
         stack.enter_context(tc.manual_schedule(engines=PINNED))
@@ -128,7 +129,7 @@ def tile_lstmcell_t_v_kernel(
         g0s = {}
 
         def tanh_and_square(j):
-            g0 = psum.tile([P, CH], BF16, tag="rest")
+            g0 = psum.tile([P, CH], BF16, tag="rest", bufs=3)
             transpose_slices(g0, lambda s: g0_nat[:, j * SL + s, :], ident_b)
             tanh_c = p2.tile([P, CH], F32, bufs=LATE_OUT + 1)
             nc.scalar.activation(
@@ -182,7 +183,7 @@ def tile_lstmcell_t_v_kernel(
                     gate[kind] = p1.tile([P, CH], F32, name="gate%d" % kind, bufs=LATE_FACTORS)
                     func = ACT.Tanh if kind == G_ else ACT.Sigmoid
                     nc.scalar.activation(out=gate[kind][:], in_=z[:], func=func)
-                cg = psum.tile([P, 2, CH], BF16, tag="rest")
+                cg = psum.tile([P, 2, CH], BF16, tag="rest", bufs=3)
                 transpose_slices(cg[:, 0, :], lambda s: c_nat[:, s, :], ident_b)
                 transpose_slices(cg[:, 1, :], lambda s: g1_nat[:, s, :], ident_b)
                 f_sq = p1.tile([P, CH], F32)
@@ -290,6 +291,23 @@ def tile_lstmcell_t_v_kernel(
             half = xh_lo if row < ROWS // 2 else xh_hi
             return half[:, row % (ROWS // 2), kind * HID : (kind + 1) * HID]
 
+        corr = psum.tile([P, HID], F32, tag="corr", bufs=1)
+
+        def out_gate_sum(j):
+            turned = psum.tile([P, SL, HID], F32, tag="rest", bufs=3)
+            for s in range(SL):
+                nc.tensor.transpose(turned[:, s, :], fac[:, O_, j * CH + s * P : j * CH + (s + 1) * P], ident_f[:])
+            rows = late.tile([P, SL, HID], F32, bufs=2)
+            nc.scalar.copy(out=rows[:], in_=turned[:])
+            for s in range(SL):
+                done.append(j * SL + s)
+                nc.tensor.matmul(
+                    out=corr[:], lhsT=rows[:, s, :], rhs=xhat_block(j * SL + s, O_),
+                    start=(len(done) == 1), stop=(len(done) == ROWS),
+                )
+
+        done = []
+
         def xhat_transposed(j, kind):
             xt = psum.tile([P, CH], F32, tag="wide")
             transpose_slices(xt, lambda s: xhat_block(j * SL + s, kind), ident_f)
@@ -306,6 +324,8 @@ def tile_lstmcell_t_v_kernel(
             else:
                 out_gate(NCH - 5)
             dcn_with_cell(j)
+            if j < NCH - LATE_OUT:
+                out_gate_sum(j)
 
         out_gate(NCH - 4)
         tot2 = small.tile([P, 2], F32)
@@ -344,7 +364,10 @@ def tile_lstmcell_t_v_kernel(
                 )
 
             def sums_with_xhat(j):
-                for kind in (O_, F_, I_, G_):
+                if j == NCH - 2:
+                    junk = p2.tile([P, HID], BF16)
+                    stt(junk[:], corr[:], 1.0, ALU.mult, ident_f[:], ALU.mult, parts3[:, KINDS + O_, 0:1])
+                for kind in (F_, I_, G_):
                     if j == NCH - 1 and kind == I_:
                         quantise_weights_copy()
                     xt = xhat_transposed(j, kind)
@@ -360,6 +383,8 @@ def tile_lstmcell_t_v_kernel(
                 if j + 1 < NCH:
                     dv_and_products(j + 1)
                 sums_with_xhat(j)
+                if j < LATE_OUT:
+                    out_gate_sum(NCH - LATE_OUT + j)
                 if j + 1 < NCH:
                     forget_product(j + 1)
 
@@ -412,7 +437,10 @@ def tile_lstmcell_t_v_kernel(
                 sums[j] = []
                 for s in range(SL):
                     rows = slice(s * P, (s + 1) * P)
-                    acc = psum.tile([P, WIDTH], F32, tag="rest")
+                    if s < SL - 1:
+                        acc = psum.tile([P, WIDTH], F32, tag="rest", bufs=3)
+                    else:
+                        acc = psum.tile([P, WIDTH], F32, tag="corr", bufs=1)
                     nc.tensor.matmul_mx(
                         out=acc[:],
                         lhsT=codes[:, rows].bitcast(E5M2X4),

@@ -349,6 +349,8 @@ def tile_lstmcell_t_v_kernel(
                 stt(dv[:], dcn[:, cols], a_tc[:, 0:1], ALU.mult, dv[:], ALU.add)
                 dvs[j] = dv
                 for kind in (I_, G_):
+                    if kind == G_ and j % 2 == 1:
+                        continue
                     raw = p3.tile([P, CH], F32, name="raw%d" % kind)
                     nc.gpsimd.tensor_tensor(out=raw[:], in0=dv[:], in1=fac[:, kind, cols], op=ALU.mult)
                     nc.scalar.activation(
@@ -356,20 +358,20 @@ def tile_lstmcell_t_v_kernel(
                         scale=gain_neg[:, kind : kind + 1], accum_out=parts3[:, kind, j : j + 1],
                     )
 
-            def forget_product(j):
+            def vector_products(j):
                 cols = columns(j)
-                stt(
-                    fac[:, F_, cols], dvs[j][:], gain_neg[:, F_ : F_ + 1], ALU.mult, fac[:, F_, cols], ALU.mult,
-                    parts3[:, F_, j : j + 1],
-                )
+                for kind in (F_, G_):
+                    if kind == G_ and j % 2 == 0:
+                        continue
+                    stt(
+                        fac[:, kind, cols], dvs[j][:], gain_neg[:, kind : kind + 1], ALU.mult, fac[:, kind, cols],
+                        ALU.mult, parts3[:, kind, j : j + 1],
+                    )
+                waiting.extend([(F_, j), (I_, j), (G_, j)])
 
-            def sums_with_xhat(j):
-                if j == NCH - 2:
-                    junk = p2.tile([P, HID], BF16)
-                    stt(junk[:], corr[:], 1.0, ALU.mult, ident_f[:], ALU.mult, parts3[:, KINDS + O_, 0:1])
-                for kind in (F_, I_, G_):
-                    if j == NCH - 1 and kind == I_:
-                        quantise_weights_copy()
+            def sums_with_xhat(count):
+                for kind, j in waiting[0:count]:
+                    waiting.remove((kind, j))
                     xt = xhat_transposed(j, kind)
                     junk = p2.tile([P, CH], BF16)
                     stt(
@@ -377,16 +379,19 @@ def tile_lstmcell_t_v_kernel(
                         parts3[:, KINDS + kind, j : j + 1],
                     )
 
-            dv_and_products(0)
-            forget_product(0)
+            waiting = []
             for j in range(NCH):
-                if j + 1 < NCH:
-                    dv_and_products(j + 1)
-                sums_with_xhat(j)
-                if j < LATE_OUT:
-                    out_gate_sum(NCH - LATE_OUT + j)
-                if j + 1 < NCH:
-                    forget_product(j + 1)
+                dv_and_products(j)
+                sums_with_xhat(4 if j % 2 == 0 else 2)
+                if 0 < j <= LATE_OUT:
+                    out_gate_sum(NCH - LATE_OUT + j - 1)
+                vector_products(j)
+            sums_with_xhat(1)
+            junk = p2.tile([P, HID], BF16)
+            stt(junk[:], corr[:], 1.0, ALU.mult, ident_f[:], ALU.mult, parts3[:, KINDS + O_, 0:1])
+            sums_with_xhat(1)
+            quantise_weights_copy()
+            sums_with_xhat(2)
 
             quantise_weights()
             tot3 = small.tile([P, 2 * KINDS], F32)

@@ -129,15 +129,19 @@ def tile_lstmcell_t_v_kernel(
         g0s = {}
 
         def tanh_and_square(j):
-            g0 = psum.tile([P, CH], BF16, tag="rest", bufs=3)
-            transpose_slices(g0, lambda s: g0_nat[:, j * SL + s, :], ident_b)
-            tanh_c = p2.tile([P, CH], F32, bufs=LATE_OUT + 1)
+            pool = p2 if j < 2 else late
+            tanh_c = pool.tile([P, CH], F32, bufs=2 if j < 2 else NCH - 2)
             nc.scalar.activation(
                 out=tanh_c[:], in_=cell[:, columns(j)], func=ACT.Tanh, bias=b_tc[:, 0:1], scale=a_tc[:, 0:1]
             )
-            through = p2.tile([P, CH], F32)
+            through = pool.tile([P, CH], F32, bufs=2 if j < 2 else 4)
             nc.scalar.activation(out=through[:], in_=tanh_c[:], func=ACT.Square)
-            tanhs[j], throughs[j], g0s[j] = tanh_c, through, g0
+            tanhs[j], throughs[j] = tanh_c, through
+
+        def g0_transposed(j):
+            g0 = psum.tile([P, CH], BF16, tag="rest", bufs=3)
+            transpose_slices(g0, lambda s: g0_nat[:, j * SL + s, :], ident_b)
+            g0s[j] = g0
 
         def through_tanh(j):
             stt(throughs[j][:], throughs[j][:], 1.0, ALU.subtract, dcn[:, columns(j)], ALU.mult)
@@ -149,13 +153,22 @@ def tile_lstmcell_t_v_kernel(
                 parts3[:, O_, j : j + 1],
             )
 
+        def out_gate_gpsimd(j, scratch):
+            cols = columns(j)
+            nc.gpsimd.tensor_tensor(out=scratch[:], in0=tanhs[j][:], in1=fac[:, O_, cols], op=ALU.mult)
+            nc.scalar.activation(
+                out=fac[:, O_, cols], in_=scratch[:], func=ACT.Identity,
+                scale=gain_neg[:, O_ : O_ + 1], accum_out=parts3[:, O_, j : j + 1],
+            )
+
         def dcn_value(j):
             stt(dcn[:, columns(j)], throughs[j][:], -1.0, ALU.mult, g0s[j][:], ALU.add, parts2[:, 0, j : j + 1])
 
         def dcn_with_cell(j):
             cols = columns(j)
-            junk = p2.tile([P, CH], BF16)
-            stt(junk[:], cell[:, cols], mean_neg[:, 0:1], ALU.add, dcn[:, cols], ALU.mult, parts2[:, 1, j : j + 1])
+            scratch = late.tile([P, CH], F32, bufs=2)
+            stt(scratch[:], cell[:, cols], mean_neg[:, 0:1], ALU.add, dcn[:, cols], ALU.mult, parts2[:, 1, j : j + 1])
+            return scratch
 
         with tc.tile_pool(name="p1", bufs=2) as p1:
             acts = {}
@@ -275,6 +288,7 @@ def tile_lstmcell_t_v_kernel(
             factor(O_, last)
             stt(b_tc[:], mean_neg[:], a_tc[:, 0:1], ALU.mult, beta_c, ALU.add)
             tanh_and_square(0)
+            tanh_and_square(1)
             rstd_sq = small.tile([P, 1], F32)
             nc.vector.tensor_tensor(out=rstd_sq[:], in0=rstd[:], in1=rstd[:], op=ALU.mult)
             nc.vector.tensor_scalar_mul(out=coef2[:, 0:1], in0=a_tc[:], scalar1=-1.0 / BATCH)
@@ -313,19 +327,25 @@ def tile_lstmcell_t_v_kernel(
             transpose_slices(xt, lambda s: xhat_block(j * SL + s, kind), ident_f)
             return xt
 
-        through_tanh(0)
-        for j in range(NCH):
-            if j < NCH - LATE_OUT:
-                out_gate(j)
-            dcn_value(j)
-            if j + 1 < NCH:
-                tanh_and_square(j + 1)
-                through_tanh(j + 1)
-            else:
-                out_gate(NCH - 5)
-            dcn_with_cell(j)
-            if j < NCH - LATE_OUT:
-                out_gate_sum(j)
+        for n in range(NCH // 2):
+            first, second = 2 * n, 2 * n + 1
+            g0_transposed(first)
+            g0_transposed(second)
+            through_tanh(first)
+            through_tanh(second)
+            if n + 1 < NCH // 2:
+                tanh_and_square(first + 2)
+                tanh_and_square(second + 2)
+            if n > 0:
+                dcn_with_cell(first - 2)
+                out_gate_gpsimd(n - 1, dcn_with_cell(second - 2))
+            dcn_value(first)
+            dcn_value(second)
+            if n > 0:
+                out_gate_sum(n - 1)
+        out_gate(NCH - 5)
+        dcn_with_cell(NCH - 2)
+        dcn_with_cell(NCH - 1)
 
         out_gate(NCH - 4)
         tot2 = small.tile([P, 2], F32)

from contextlib import ExitStack

import concourse.mybir as mybir
from concourse.masks import make_identity

F32 = mybir.dt.float32
BF16 = mybir.dt.bfloat16
U32 = mybir.dt.uint32
U8 = mybir.dt.uint8
E4M3X4 = mybir.dt.float8_e4m3fn_x4
E5M2X4 = mybir.dt.float8_e5m2_x4
ACT = mybir.ActivationFunctionType
ALU = mybir.AluOpType
AX = mybir.AxisListType

P = 128
BATCH = 4096
HID = 128
KINDS = 4
GATES = KINDS * HID
WIDTH = 512
ROWS = BATCH // P
SL = 4
CH = SL * P
NCH = ROWS // SL
EPS = 1e-5
F_, I_, O_, G_ = 0, 1, 2, 3
LATE_FACTORS = 3
LATE_OUT = 5
PINNED = {mybir.EngineType.DVE, mybir.EngineType.Pool}

FLOPS = 2 * BATCH * GATES * WIDTH
BYTES = 4 * 3 * BATCH * GATES + 2 * 3 * BATCH * HID + 2 * GATES * WIDTH + 6 * GATES + 4 * HID


def tile_lstmcell_t_v_kernel(
    tc, x, c, h, w_ih, w_hh, b, g_ih, b_ih, g_hh, b_hh, g_c, b_c, gates, ih_hat, ih_rstd, grad_out, out
):
    nc = tc.nc
    gates_v = gates.rearrange("(p t) k -> p t k", t=ROWS)
    xhat_v = ih_hat.rearrange("(p t) k -> p t k", t=ROWS)
    c_v = c.rearrange("(p t) k -> p t k", t=ROWS)
    grad_v = grad_out.rearrange("s (p t) k -> p s t k", t=ROWS)
    out_v = out.rearrange("(p t) k -> p t k", t=ROWS)

    def stt(out_ap, in0, scalar, op0, in1, op1, accum=None):
        nc.vector.scalar_tensor_tensor(
            out=out_ap, in0=in0, scalar=scalar, in1=in1, op0=op0, op1=op1, accum_out=accum
        )

    def transpose_slices(dst, src_of_slice, ident):
        for s in range(SL):
            nc.tensor.transpose(dst[:, s * P : (s + 1) * P], src_of_slice(s), ident[:])

    with ExitStack() as stack:
        keep = stack.enter_context(tc.tile_pool(name="keep", bufs=1))
        psum = stack.enter_context(tc.psum_pool(name="psum", bufs=4))

        ident_f = keep.tile([P, P], F32)
        make_identity(nc, ident_f[:])
        ident_b = keep.tile([P, P], BF16)
        make_identity(nc, ident_b[:])
        rows_b = keep.tile([P, P], BF16)
        nc.vector.memset(rows_b[:], 0.0)
        rows_f = keep.tile([P, P], F32)
        nc.vector.memset(rows_f[:], 0.0)
        neg_half = keep.tile([P, 1], F32)
        nc.vector.memset(neg_half[:], -0.5)
        warm = keep.tile([P, 1], F32)
        nc.scalar.dma_start(out=rows_b[0:KINDS, :], in_=g_ih.rearrange("(t p) -> t p", p=P))
        nc.scalar.dma_start(out=rows_b[4:5, :], in_=g_c.rearrange("(o p) -> o p", o=1))
        nc.scalar.dma_start(out=rows_b[5:6, :], in_=b_c.rearrange("(o p) -> o p", o=1))
        nc.scalar.dma_start(out=rows_f[0:KINDS, :], in_=ih_rstd.rearrange("(t p) -> t p", p=P))
        nc.scalar.activation(out=warm[:], in_=neg_half[:], func=ACT.Sigmoid)

        cols_b = psum.tile([P, P], BF16, tag="rest", bufs=3)
        nc.tensor.transpose(cols_b[:], rows_b[:], ident_b[:])
        cols_f = psum.tile([P, P], F32, tag="wide")
        nc.tensor.transpose(cols_f[:], rows_f[:], ident_f[:])
        vecs = keep.tile([P, 6], F32)
        nc.vector.tensor_copy(out=vecs[:], in_=cols_b[:, 0:6])
        gamma_c = vecs[:, 4:5]
        beta_c = vecs[:, 5:6]
        gain_neg = keep.tile([P, KINDS], F32)
        stt(gain_neg[:], vecs[:, 0:KINDS], -1.0, ALU.mult, cols_f[:, 0:KINDS], ALU.mult)

        fac = keep.tile([P, KINDS, BATCH], F32)
        xh_lo = keep.tile([P, ROWS // 2, GATES], F32)
        cell = keep.tile([P, BATCH], F32)
        dcn = keep.tile([P, BATCH], F32)
        g0_nat = keep.tile([P, ROWS, HID], BF16)
        w_nat = keep.tile([P, KINDS, WIDTH], BF16)
        w_grouped = keep.tile([P, WIDTH, KINDS], BF16, align_bytes=64)
        w_codes = keep.tile([P, WIDTH], U32, align_bytes=64)
        w_scales = keep.tile([P, WIDTH], U8, align_bytes=64)
        sum_v = keep.tile([P, NCH], F32)
        sq_parts = keep.tile([P, NCH], F32)
        parts2 = keep.tile([P, 2, NCH], F32)
        parts3 = keep.tile([P, 2 * KINDS, NCH], F32)
        shift_neg = keep.tile([P, 1], F32)
        mean_neg = keep.tile([P, 1], F32)
        a_tc = keep.tile([P, 1], F32)
        b_tc = keep.tile([P, 1], F32)
        coef2 = keep.tile([P, 2], F32)
        lin2 = keep.tile([P, 2], F32)
        c_lin = keep.tile([P, 1], F32)
        neg3 = keep.tile([P, 2 * KINDS], F32)
        nc.vector.memset(parts3[:, KINDS + O_, :], 0.0)
        small = stack.enter_context(tc.tile_pool(name="small", bufs=1))
        p2 = stack.enter_context(tc.tile_pool(name="p2", bufs=2))
        stack.enter_context(tc.manual_schedule(engines=PINNED))

        def columns(j):
            return slice(j * CH, (j + 1) * CH)

        def quantise_weights_copy():
            nc.vector.tensor_copy(
                out=w_grouped[:].rearrange("p (c i) t -> p c t i", i=4),
                in_=w_nat[:].rearrange("p t (c i) -> p c t i", i=4),
            )

        def quantise_weights():
            nc.vector.quantize_mx(
                out=w_codes[:].bitcast(E4M3X4), scales=w_scales[:], in_=w_grouped[:].rearrange("p i t -> p (i t)")
            )

        tanhs = {}
        throughs = {}
        g0s = {}

        def tanh_and_square(j):
            pool = p2 if j < 2 else late
            tanh_c = pool.tile([P, CH], F32, bufs=2 if j < 2 else NCH - 2)
            nc.scalar.activation(
                out=tanh_c[:], in_=cell[:, columns(j)], func=ACT.Tanh, bias=b_tc[:, 0:1], scale=a_tc[:, 0:1]
            )
            through = pool.tile([P, CH], F32, bufs=2 if j < 2 else 4)
            nc.scalar.activation(out=through[:], in_=tanh_c[:], func=ACT.Square)
            tanhs[j], throughs[j] = tanh_c, through

        def g0_transposed(j):
            g0 = psum.tile([P, CH], BF16, tag="rest", bufs=3)
            transpose_slices(g0, lambda s: g0_nat[:, j * SL + s, :], ident_b)
            g0s[j] = g0

        def through_tanh(j):
            stt(throughs[j][:], throughs[j][:], 1.0, ALU.subtract, dcn[:, columns(j)], ALU.mult)

        def out_gate(j):
            cols = columns(j)
            stt(
                fac[:, O_, cols], tanhs[j][:], gain_neg[:, O_ : O_ + 1], ALU.mult, fac[:, O_, cols], ALU.mult,
                parts3[:, O_, j : j + 1],
            )

        def out_gate_gpsimd(j, scratch):
            cols = columns(j)
            nc.gpsimd.tensor_tensor(out=scratch[:], in0=tanhs[j][:], in1=fac[:, O_, cols], op=ALU.mult)
            nc.scalar.activation(
                out=fac[:, O_, cols], in_=scratch[:], func=ACT.Identity,
                scale=gain_neg[:, O_ : O_ + 1], accum_out=parts3[:, O_, j : j + 1],
            )

        def dcn_value(j):
            stt(dcn[:, columns(j)], throughs[j][:], -1.0, ALU.mult, g0s[j][:], ALU.add, parts2[:, 0, j : j + 1])

        def dcn_with_cell(j):
            cols = columns(j)
            scratch = late.tile([P, CH], F32, bufs=2)
            stt(scratch[:], cell[:, cols], mean_neg[:, 0:1], ALU.add, dcn[:, cols], ALU.mult, parts2[:, 1, j : j + 1])
            return scratch

        with tc.tile_pool(name="p1", bufs=2) as p1:
            acts = {}

            def load_and_activate(j):
                sl = slice(j * SL, (j + 1) * SL)
                z_nat = p1.tile([P, SL, GATES], F32, bufs=3)
                c_nat = p1.tile([P, SL, HID], BF16, bufs=3)
                g1_nat = p1.tile([P, SL, HID], BF16, bufs=3)
                if j == 0:
                    for kind in (F_, I_, G_, O_):
                        ks = slice(kind * HID, (kind + 1) * HID)
                        nc.sync.dma_start(out=z_nat[:, :, ks], in_=gates_v[:, sl, ks])
                        if kind == F_:
                            nc.sync.dma_start(out=c_nat[:], in_=c_v[:, sl, :])
                    nc.sync.dma_start(out=g1_nat[:], in_=grad_v[:, 1, sl, :])
                else:
                    nc.sync.dma_start(out=z_nat[:], in_=gates_v[:, sl, :])
                    nc.sync.dma_start(out=c_nat[:], in_=c_v[:, sl, :])
                    nc.sync.dma_start(out=g1_nat[:], in_=grad_v[:, 1, sl, :])
                gate = {}
                for kind in (F_, I_, G_, O_):
                    z = psum.tile([P, CH], F32, tag="wide")
                    transpose_slices(z, lambda s: z_nat[:, s, kind * HID : (kind + 1) * HID], ident_f)
                    gate[kind] = p1.tile([P, CH], F32, name="gate%d" % kind, bufs=LATE_FACTORS)
                    func = ACT.Tanh if kind == G_ else ACT.Sigmoid
                    nc.scalar.activation(out=gate[kind][:], in_=z[:], func=func)
                cg = psum.tile([P, 2, CH], BF16, tag="rest", bufs=3)
                transpose_slices(cg[:, 0, :], lambda s: c_nat[:, s, :], ident_b)
                transpose_slices(cg[:, 1, :], lambda s: g1_nat[:, s, :], ident_b)
                f_sq = p1.tile([P, CH], F32)
                nc.scalar.activation(out=f_sq[:], in_=gate[F_][:], func=ACT.Square, bias=neg_half[:, 0:1])
                g_sq = p1.tile([P, CH], F32, bufs=LATE_FACTORS)
                nc.scalar.activation(out=g_sq[:], in_=gate[G_][:], func=ACT.Square)
                ig = p1.tile([P, CH], F32, bufs=1)
                nc.gpsimd.tensor_tensor(out=ig[:], in0=gate[I_][:], in1=gate[G_][:], op=ALU.mult)
                acts[j] = (gate, f_sq, g_sq, ig, cg)

            def psum_products(j):
                cols = columns(j)
                gate, f_sq, g_sq, ig, cg = acts[j]
                nc.vector.tensor_tensor(out=cell[:, cols], in0=gate[F_][:], in1=cg[:, 0, :], op=ALU.mult)
                nc.vector.tensor_tensor(out=dcn[:, cols], in0=gate[O_][:], in1=cg[:, 1, :], op=ALU.mult)
                stt(fac[:, F_, cols], f_sq[:], 0.25, ALU.subtract, cg[:, 0, :], ALU.mult)

            def cell_sum(j):
                cols = columns(j)
                ig = acts[j][3]
                stt(cell[:, cols], cell[:, cols], 1.0, ALU.mult, ig[:], ALU.add, sum_v[:, j : j + 1])
                if j == 0:
                    nc.vector.tensor_scalar_mul(out=shift_neg[:], in0=sum_v[:, 0:1], scalar1=-1.0 / CH)
                sq_junk = p1.tile([P, CH], BF16)
                nc.scalar.activation(
                    out=sq_junk[:], in_=cell[:, cols], func=ACT.Square,
                    bias=shift_neg[:, 0:1], scale=1.0, accum_out=sq_parts[:, j : j + 1],
                )

            def factor(kind, j):
                cols = columns(j)
                gate, f_sq, g_sq, ig, cg = acts[j]
                if kind == G_:
                    stt(fac[:, G_, cols], g_sq[:], 1.0, ALU.subtract, gate[I_][:], ALU.mult)
                elif kind == O_:
                    stt(fac[:, O_, cols], gate[O_][:], 1.0, ALU.subtract, dcn[:, cols], ALU.mult)
                else:
                    stt(fac[:, I_, cols], gate[I_][:], 1.0, ALU.subtract, ig[:], ALU.mult)

            last = NCH - 1
            for j in range(last):
                load_and_activate(j)
                psum_products(j)
                cell_sum(j)
                if j < NCH - LATE_FACTORS:
                    factor(G_, j)
                    factor(O_, j)
                factor(I_, j)

            sum_early = small.tile([P, 1], F32)
            nc.vector.reduce_sum(out=sum_early[:], in_=sum_v[:, 0:last], axis=AX.X)
            load_and_activate(last)
            psum_products(last)
            dev_early = small.tile([P, 1], F32)
            stt(dev_early[:], shift_neg[:], float(BATCH), ALU.mult, sum_early[:], ALU.add)
            sq_early = small.tile([P, 1], F32)
            nc.vector.reduce_sum(out=sq_early[:], in_=sq_parts[:, 0:last], axis=AX.X)
            cell_sum(last)

            nc.sync.dma_start(out=g0_nat[:], in_=grad_v[:, 0, :, :])
            nc.sync.dma_start(out=w_nat[:], in_=w_ih.rearrange("(t p) i -> p t i", p=P))
            for j in range(NCH // 2):
                sl = slice(j * SL, (j + 1) * SL)
                nc.sync.dma_start(out=xh_lo[:, sl, :], in_=xhat_v[:, sl, :])

            spread_early = small.tile([P, 1], F32)
            nc.vector.tensor_scalar(
                out=spread_early[:], in0=sq_early[:], scalar1=1.0 / BATCH, scalar2=EPS, op0=ALU.mult, op1=ALU.add
            )
            factor(G_, last - 2)
            dev = small.tile([P, 1], F32)
            nc.vector.tensor_tensor(out=dev[:], in0=dev_early[:], in1=sum_v[:, last : last + 1], op=ALU.add)
            factor(O_, last - 2)
            dev_sq_neg = small.tile([P, 1], F32)
            stt(dev_sq_neg[:], dev[:], -1.0 / (BATCH * BATCH), ALU.mult, dev[:], ALU.mult)
            nc.vector.tensor_scalar(
                out=mean_neg[:], in0=dev[:], scalar1=-1.0 / BATCH, scalar2=shift_neg[:, 0:1], op0=ALU.mult, op1=ALU.add
            )
            spread = small.tile([P, 1], F32)
            stt(spread[:], sq_parts[:, last : last + 1], 1.0 / BATCH, ALU.mult, spread_early[:], ALU.add)
            factor(G_, last - 1)
            var_eps = small.tile([P, 1], F32)
            nc.vector.tensor_tensor(out=var_eps[:], in0=spread[:], in1=dev_sq_neg[:], op=ALU.add)
            rstd = small.tile([P, 1], F32)
            nc.gpsimd.tensor_tensor(out=rstd[:], in0=var_eps[:], in1=neg_half[:], op=ALU.pow)
            factor(O_, last - 1)
            factor(G_, last)
            nc.vector.tensor_tensor(out=a_tc[:], in0=rstd[:], in1=gamma_c, op=ALU.mult)
            factor(O_, last)
            stt(b_tc[:], mean_neg[:], a_tc[:, 0:1], ALU.mult, beta_c, ALU.add)
            tanh_and_square(0)
            tanh_and_square(1)
            rstd_sq = small.tile([P, 1], F32)
            nc.vector.tensor_tensor(out=rstd_sq[:], in0=rstd[:], in1=rstd[:], op=ALU.mult)
            nc.vector.tensor_scalar_mul(out=coef2[:, 0:1], in0=a_tc[:], scalar1=-1.0 / BATCH)
            factor(I_, last)
            nc.vector.tensor_tensor(out=coef2[:, 1:2], in0=coef2[:, 0:1], in1=rstd_sq[:], op=ALU.mult)

        late = stack.enter_context(tc.tile_pool(name="late", bufs=1, reuse_waits="tile"))
        xh_hi = late.tile([P, ROWS // 2, GATES], F32)
        for j in range(NCH // 2):
            sl = slice(j * SL, (j + 1) * SL)
            nc.sync.dma_start(out=xh_hi[:, sl, :], in_=xhat_v[:, ROWS // 2 + j * SL : ROWS // 2 + (j + 1) * SL, :])

        def xhat_block(row, kind):
            half = xh_lo if row < ROWS // 2 else xh_hi
            return half[:, row % (ROWS // 2), kind * HID : (kind + 1) * HID]

        corr = psum.tile([P, HID], F32, tag="corr", bufs=1)

        def out_gate_sum(j):
            turned = psum.tile([P, SL, HID], F32, tag="rest", bufs=3)
            for s in range(SL):
                nc.tensor.transpose(turned[:, s, :], fac[:, O_, j * CH + s * P : j * CH + (s + 1) * P], ident_f[:])
            rows = late.tile([P, SL, HID], F32, bufs=2)
            nc.scalar.copy(out=rows[:], in_=turned[:])
            for s in range(SL):
                done.append(j * SL + s)
                nc.tensor.matmul(
                    out=corr[:], lhsT=rows[:, s, :], rhs=xhat_block(j * SL + s, O_),
                    start=(len(done) == 1), stop=(len(done) == ROWS),
                )

        done = []

        def xhat_transposed(j, kind):
            xt = psum.tile([P, CH], F32, tag="wide")
            transpose_slices(xt, lambda s: xhat_block(j * SL + s, kind), ident_f)
            return xt

        for n in range(NCH // 2):
            first, second = 2 * n, 2 * n + 1
            g0_transposed(first)
            g0_transposed(second)
            through_tanh(first)
            through_tanh(second)
            if n + 1 < NCH // 2:
                tanh_and_square(first + 2)
                tanh_and_square(second + 2)
            if n > 0:
                dcn_with_cell(first - 2)
                out_gate_gpsimd(n - 1, dcn_with_cell(second - 2))
            dcn_value(first)
            dcn_value(second)
            if n > 0:
                out_gate_sum(n - 1)
        out_gate(NCH - 5)
        dcn_with_cell(NCH - 2)
        dcn_with_cell(NCH - 1)

        out_gate(NCH - 4)
        tot2 = small.tile([P, 2], F32)
        nc.vector.reduce_sum(out=tot2[:], in_=parts2[:], axis=AX.X)
        out_gate(NCH - 3)
        nc.vector.tensor_tensor(out=lin2[:], in0=tot2[:], in1=coef2[:], op=ALU.mult)
        out_gate(NCH - 2)
        stt(c_lin[:], lin2[:, 1:2], mean_neg[:, 0:1], ALU.mult, lin2[:, 0:1], ALU.add)

        with tc.tile_pool(name="p3", bufs=2, reuse_waits="tile") as p3:
            dvs = {}

            def dv_and_products(j):
                cols = columns(j)
                dv = p3.tile([P, CH], F32)
                nc.scalar.activation(
                    out=dv[:], in_=cell[:, cols], func=ACT.Identity, bias=c_lin[:, 0:1], scale=lin2[:, 1:2]
                )
                if j == 0:
                    out_gate(NCH - 1)
                stt(dv[:], dcn[:, cols], a_tc[:, 0:1], ALU.mult, dv[:], ALU.add)
                dvs[j] = dv
                for kind in (I_, G_):
                    if kind == G_ and j % 2 == 1:
                        continue
                    raw = p3.tile([P, CH], F32, name="raw%d" % kind)
                    nc.gpsimd.tensor_tensor(out=raw[:], in0=dv[:], in1=fac[:, kind, cols], op=ALU.mult)
                    nc.scalar.activation(
                        out=fac[:, kind, cols], in_=raw[:], func=ACT.Identity,
                        scale=gain_neg[:, kind : kind + 1], accum_out=parts3[:, kind, j : j + 1],
                    )

            def vector_products(j):
                cols = columns(j)
                for kind in (F_, G_):
                    if kind == G_ and j % 2 == 0:
                        continue
                    stt(
                        fac[:, kind, cols], dvs[j][:], gain_neg[:, kind : kind + 1], ALU.mult, fac[:, kind, cols],
                        ALU.mult, parts3[:, kind, j : j + 1],
                    )
                waiting.extend([(F_, j), (I_, j), (G_, j)])

            def sums_with_xhat(count):
                for kind, j in waiting[0:count]:
                    waiting.remove((kind, j))
                    xt = xhat_transposed(j, kind)
                    junk = p2.tile([P, CH], BF16)
                    stt(
                        junk[:], fac[:, kind, columns(j)], 1.0, ALU.mult, xt[:], ALU.mult,
                        parts3[:, KINDS + kind, j : j + 1],
                    )

            waiting = []
            for j in range(NCH):
                dv_and_products(j)
                sums_with_xhat(4 if j % 2 == 0 else 2)
                if 0 < j <= LATE_OUT:
                    out_gate_sum(NCH - LATE_OUT + j - 1)
                vector_products(j)
            sums_with_xhat(1)
            junk = p2.tile([P, HID], BF16)
            stt(junk[:], corr[:], 1.0, ALU.mult, ident_f[:], ALU.mult, parts3[:, KINDS + O_, 0:1])
            sums_with_xhat(1)
            quantise_weights_copy()
            sums_with_xhat(2)

            quantise_weights()
            tot3 = small.tile([P, 2 * KINDS], F32)
            nc.vector.reduce_sum(out=tot3[:], in_=parts3[:], axis=AX.X)
            nc.vector.tensor_scalar_mul(out=neg3[:], in0=tot3[:], scalar1=-1.0 / BATCH)

        with tc.tile_pool(name="p4", bufs=2, reuse_waits="tile") as p4:
            sums = {}

            def shift_buffer(j):
                half = (j % 2) * KINDS * CH
                return dcn[:, half : half + KINDS * CH].rearrange("p (t b) -> p t b", t=KINDS)

            def result_buffer(j):
                half = (j % 2) * SL * WIDTH
                return cell[:, half : half + SL * WIDTH].rearrange("p (s i) -> p s i", s=SL)

            def shift_terms(j):
                for kind in range(KINDS):
                    xt = xhat_transposed(j, kind)
                    if j == 0 and kind >= 2:
                        nc.vector.tensor_scalar(
                            out=shift_buffer(j)[:, kind, :], in0=xt[:], scalar1=neg3[:, KINDS + kind : KINDS + kind + 1],
                            scalar2=neg3[:, kind : kind + 1], op0=ALU.mult, op1=ALU.add,
                        )
                    else:
                        nc.scalar.activation(
                            out=shift_buffer(j)[:, kind, :], in_=xt[:], func=ACT.Identity,
                            bias=neg3[:, kind : kind + 1], scale=neg3[:, KINDS + kind : KINDS + kind + 1],
                        )

            def add_and_round(j):
                da = p4.tile([P, CH, KINDS], BF16, align_bytes=64)
                nc.vector.tensor_tensor(
                    out=da[:].rearrange("p (c i) t -> p c t i", i=4),
                    in0=fac[:, :, columns(j)].rearrange("p t (c i) -> p c t i", i=4),
                    in1=shift_buffer(j).rearrange("p t (c i) -> p c t i", i=4),
                    op=ALU.add,
                )
                return da

            def quantise_and_multiply(j, da):
                codes = p4.tile([P, CH], U32, align_bytes=64)
                scales = p4.tile([P, CH], U8, align_bytes=64)
                nc.vector.quantize_mx(
                    out=codes[:].bitcast(E5M2X4), scales=scales[:], in_=da[:].rearrange("p b t -> p (b t)")
                )
                sums[j] = []
                for s in range(SL):
                    rows = slice(s * P, (s + 1) * P)
                    if s < SL - 1:
                        acc = psum.tile([P, WIDTH], F32, tag="rest", bufs=3)
                    else:
                        acc = psum.tile([P, WIDTH], F32, tag="corr", bufs=1)
                    nc.tensor.matmul_mx(
                        out=acc[:],
                        lhsT=codes[:, rows].bitcast(E5M2X4),
                        lhsT_scale=scales[:, rows],
                        rhs=w_codes[:].bitcast(E4M3X4),
                        rhs_scale=w_scales[:],
                        start=True,
                        stop=True,
                    )
                    sums[j].append(acc)

            def store(j):
                result = result_buffer(j)
                for s in range(SL):
                    if s % 2 == 0 or (s == 1 and j % 2 == 1):
                        nc.scalar.copy(out=result[:, s, :], in_=sums[j][s][:])
                    else:
                        nc.vector.tensor_copy(out=result[:, s, :], in_=sums[j][s][:])
                    if j == NCH - 1:
                        nc.sync.dma_start(out=out_v[:, j * SL + s, :], in_=result[:, s, :])
                if j < NCH - 1:
                    nc.sync.dma_start(out=out_v[:, j * SL : (j + 1) * SL, :], in_=result)

            shift_terms(0)
            for j in range(NCH + 1):
                if j + 1 < NCH:
                    shift_terms(j + 1)
                if j < NCH:
                    da = add_and_round(j)
                if j > 0:
                    store(j - 1)
                if j < NCH:
                    quantise_and_multiply(j, da)
